import numpy as np
import ml_dtypes


def mxq(x, axis, fmt="e4m3"):
    dtype, down = {"e4m3": (ml_dtypes.float8_e4m3fn, 7), "e5m2": (ml_dtypes.float8_e5m2, 14)}[fmt]
    v = np.moveaxis(np.asarray(x, np.float32).astype(ml_dtypes.bfloat16).astype(np.float64), axis, -1)
    blocks = v.reshape(v.shape[:-1] + (-1, 32))
    amax = np.abs(blocks).max(-1, keepdims=True)
    byte = np.maximum(np.where(amax > 0, np.frexp(amax)[1] - 1 + 127, 0) - down, 1)
    scale = np.exp2(byte - 127.0)
    codes = (blocks / scale).astype(np.float32).astype(dtype).astype(np.float64)
    return np.moveaxis((codes * scale).reshape(v.shape), -1, axis)


WIDE = False


def mx_kscale(k):
    if not WIDE:
        return np.ones(k)
    levels = np.array([10, -10, 5, -5, 0])
    a = np.random.permutation(np.resize(levels, k // 512 * 4)).reshape(k // 512, 4)
    idx = np.arange(k)
    return np.exp2(a[idx // 512, idx % 128 // 32])


BF16 = ml_dtypes.bfloat16


def bf(x):
    return np.asarray(x, np.float32).astype(BF16)


def f64(x):
    return np.asarray(x).astype(np.float64)


B, N, C = 2, 512, 1024
R = B * N
G = 3 * C


def sigmoid(v):
    return 1.0 / (1.0 + np.exp(-v))


def setup_inputs():
    s = mx_kscale(C)
    s = s / s.max()
    return {"x_proj": bf(np.random.standard_normal((R, G))),
            "annotations": bf(np.random.standard_normal((B, N, C)) * s),
            "recurrent_kernel": bf(np.random.standard_normal((C, G)) / np.sqrt(C) / s[:, None]),
            "bias_h": bf(np.random.standard_normal(G) * 0.3)}


def reference(x_proj, annotations, recurrent_kernel, bias_h):
    b, n, c = annotations.shape
    h = f64(annotations).reshape(-1, c)
    mh = (mxq(h, 1, "e4m3") @ mxq(f64(recurrent_kernel), 0, "e4m3")) + f64(bias_h)
    xz, xr, xh = np.split(f64(x_proj), 3, axis=-1)
    hz, hr, hh_in = np.split(mh, 3, axis=-1)
    z = sigmoid(xz + hz)
    r = sigmoid(xr + hr)
    hh = np.tanh(xh + r * hh_in)
    out = z * h + (1.0 - z) * hh
    return out.reshape(b, n, c)

@@ -1,0 +1,302 @@
+from contextlib import ExitStack
+
+import concourse.mybir as mybir
+from concourse.masks import make_identity
+
+F32 = mybir.dt.float32
+BF16 = mybir.dt.bfloat16
+U32 = mybir.dt.uint32
+U8 = mybir.dt.uint8
+FP8X4 = mybir.dt.float8_e4m3fn_x4
+ACT = mybir.ActivationFunctionType
+
+P = 128
+PACK = 4
+K_PASS = P * PACK
+NODES = 1024
+C = 1024
+PASSES = C // K_PASS
+HALF = 512
+TILES = HALF // P
+BLOCKS = 4
+STEPS = BLOCKS * TILES
+
+Z_GATE, R_GATE, C_GATE = 0, 1, 2
+GATE_ORDER = (R_GATE, C_GATE, Z_GATE)
+
+FLOPS = 2 * NODES * C * 3 * C
+
+LOAD_AHEAD = 4
+FIRST_ITERATION = -5 - LOAD_AHEAD
+
+
+def tile_gatedgraphconvolution_pb_kernel(
+    tc, x_proj, annotations, recurrent_kernel, bias_h, out
+):
+    nc = tc.nc
+    h_rows = annotations.flatten_outer_dims()
+    out_rows = out.flatten_outer_dims()
+
+    with ExitStack() as ctx:
+        ctx.enter_context(tc.manual_schedule())
+        const = ctx.enter_context(tc.tile_pool(name="const", bufs=1))
+        keep = ctx.enter_context(tc.tile_pool(name="keep", bufs=1))
+        w_raw_pool = ctx.enter_context(tc.tile_pool(name="w_raw", bufs=6))
+        w_grouped_pool = ctx.enter_context(tc.tile_pool(name="w_grouped", bufs=4))
+        x_pool = ctx.enter_context(tc.tile_pool(name="x", bufs=6))
+        biased_pool = ctx.enter_context(tc.tile_pool(name="biased", bufs=2))
+        gate_pool = ctx.enter_context(tc.tile_pool(name="gates", bufs=3))
+        mix_pool = ctx.enter_context(tc.tile_pool(name="mix", bufs=4))
+        product_pool = ctx.enter_context(tc.psum_pool(name="product", bufs=4))
+        turned_pool = ctx.enter_context(tc.psum_pool(name="turned", bufs=4))
+
+        ident_f32 = const.tile([P, P], F32, name="ident_f32")
+        make_identity(nc, ident_f32[:])
+        ident_bf16 = const.tile([P, P], BF16, name="ident_bf16")
+        make_identity(nc, ident_bf16[:])
+
+        warm = const.tile([P, 1], F32, name="warm")
+        nc.vector.memset(warm[:], 0.0)
+        nc.scalar.activation(out=warm[:], in_=warm[:], func=ACT.Sigmoid)
+
+        bias_tiles = 3 * C // P
+        bias_rows = const.tile([P, P], BF16, name="bias_rows")
+        nc.vector.memset(bias_rows[:], 0.0)
+        nc.sync.dma_start(
+            out=bias_rows[0:bias_tiles, :], in_=bias_h.rearrange("(j p) -> j p", p=P)
+        )
+        bias_turned = turned_pool.tile([P, P], BF16, name="bias_turned", tag="turned")
+        nc.tensor.transpose(out=bias_turned[:], in_=bias_rows[:], identity=ident_bf16[:])
+        bias_col = const.tile([P, bias_tiles], F32, name="bias_col")
+        nc.vector.tensor_copy(out=bias_col[:], in_=bias_turned[:, 0:bias_tiles])
+
+        h_sb = keep.tile([P, NODES // P, C], BF16, name="h_sb")
+        h_grouped = keep.tile([P, PASSES * NODES * PACK], BF16, name="h_grouped", align_bytes=64)
+        h_grouped_words = h_grouped[:].bitcast(F32).rearrange(
+            "p (s n u) -> p s n u", s=PASSES, u=2
+        )
+        h_grouped_values = h_grouped[:].rearrange("p (s m) -> p s m", s=PASSES)
+        h_codes = keep.tile([P, PASSES, NODES], U32, name="h_codes", align_bytes=64)
+        h_scales = keep.tile([P, PASSES, NODES], U8, name="h_scales", align_bytes=64)
+        w_chunks = 2 * 3 * PASSES
+        w_codes = keep.tile([P, w_chunks, HALF], U32, name="w_codes", align_bytes=64)
+        w_scales = keep.tile([P, w_chunks, HALF], U8, name="w_scales", align_bytes=64)
+
+        def w_chunk(col_half, g, s):
+            return (col_half * 3 + g) * PASSES + s
+
+        w_raw = {}
+        x_tiles = {}
+        products = {}
+        biased = {}
+        turned = {}
+        reset_tiles = {}
+        update_tiles = {}
+        mix_tiles = {}
+
+        def load_w(col_half, g):
+            col0 = GATE_ORDER[g] * C + col_half * HALF
+            for s in range(PASSES):
+                raw = w_raw_pool.tile([P, PACK, HALF], BF16, name="w_raw", tag="w_raw")
+                rows = recurrent_kernel[s * K_PASS : (s + 1) * K_PASS, col0 : col0 + HALF]
+                nc.sync.dma_start(out=raw[:], in_=rows.rearrange("(p t) c -> p t c", t=PACK))
+                w_raw[(col_half, g, s)] = raw
+
+        def load_h(node_half):
+            rows = h_rows[node_half * HALF : (node_half + 1) * HALF, :]
+            nc.sync.dma_start(
+                out=h_sb[:, node_half * TILES : (node_half + 1) * TILES, :],
+                in_=rows.rearrange("(t p) c -> p t c", p=P),
+            )
+
+        def load_x(k):
+            block, tile_in_half = divmod(k, TILES)
+            col_half, node_half = divmod(block, 2)
+            row0 = (node_half * TILES + tile_in_half) * P
+            x_t = x_pool.tile([P, 3, HALF], BF16, name="x_t", tag="x_t")
+            cols = x_proj[row0 : row0 + P, :].rearrange("p (g c) -> p g c", g=3)
+            nc.sync.dma_start(out=x_t[:], in_=cols[:, :, col_half * HALF : (col_half + 1) * HALF])
+            x_tiles[k] = x_t
+
+        def prepare_w(col_half, g):
+            grouped = []
+            for s in range(PASSES):
+                w_grouped = w_grouped_pool.tile(
+                    [P, HALF, PACK], BF16, name="w_grouped", tag="w_grouped", align_bytes=64
+                )
+                nc.vector.tensor_copy(
+                    out=w_grouped[:].rearrange("p (c i) t -> p c t i", i=4),
+                    in_=w_raw[(col_half, g, s)][:].rearrange("p t (c i) -> p c t i", i=4),
+                )
+                grouped.append(w_grouped)
+            for s in range(PASSES):
+                chunk = w_chunk(col_half, g, s)
+                nc.vector.quantize_mx(
+                    out=w_codes[:, chunk, :].bitcast(FP8X4),
+                    scales=w_scales[:, chunk, :],
+                    in_=grouped[s][:].rearrange("p c t -> p (c t)"),
+                )
+
+        def transpose_h(node_half):
+            for s in range(PASSES):
+                for pair in range(TILES // 2):
+                    h_turned = turned_pool.tile([P, 2, 2 * P], F32, name="h_turned", tag="turned")
+                    for j in range(2):
+                        node_tile = node_half * TILES + 2 * pair + j
+                        words = h_sb[:, node_tile, :].bitcast(F32).rearrange(
+                            "p (s w u) -> p s u w", s=PASSES, u=2
+                        )
+                        for u in range(2):
+                            nc.tensor.transpose(
+                                out=h_turned[:, u, j * P : (j + 1) * P],
+                                in_=words[:, s, u, :],
+                                identity=ident_f32[:],
+                            )
+                    node0 = node_half * HALF + pair * 2 * P
+                    nc.scalar.copy(
+                        out=h_grouped_words[:, s, node0 : node0 + 2 * P, :],
+                        in_=h_turned[:].rearrange("p u n -> p n u"),
+                    )
+
+        def quantise_h(node_half):
+            nodes = slice(node_half * HALF, (node_half + 1) * HALF)
+            for s in range(PASSES):
+                nc.vector.quantize_mx(
+                    out=h_codes[:, s, nodes].bitcast(FP8X4),
+                    scales=h_scales[:, s, nodes],
+                    in_=h_grouped_values[:, s, node_half * HALF * PACK : (node_half + 1) * HALF * PACK],
+                )
+
+        def multiply_gate(block, g):
+            col_half, node_half = divmod(block, 2)
+            nodes = slice(node_half * HALF, (node_half + 1) * HALF)
+            for ct in range(TILES):
+                cols = slice(ct * P, (ct + 1) * P)
+                product = product_pool.tile([P, HALF], F32, name="product", tag="product")
+                for s in range(PASSES):
+                    chunk = w_chunk(col_half, g, s)
+                    nc.tensor.matmul_mx(
+                        out=product[:],
+                        lhsT=w_codes[:, chunk, cols].bitcast(FP8X4),
+                        lhsT_scale=w_scales[:, chunk, cols],
+                        rhs=h_codes[:, s, nodes].bitcast(FP8X4),
+                        rhs_scale=h_scales[:, s, nodes],
+                        start=(s == 0),
+                        stop=(s == PASSES - 1),
+                    )
+                products[(block, g, ct)] = product
+
+        def add_bias(block, g):
+            col_half = block // 2
+            with_bias = biased_pool.tile(
+                [P, TILES, HALF], F32, name="with_bias", tag="with_bias_%d" % g
+            )
+            for ct in range(TILES):
+                j = GATE_ORDER[g] * (C // P) + col_half * TILES + ct
+                nc.scalar.activation(
+                    out=with_bias[:, ct, :],
+                    in_=products[(block, g, ct)][:],
+                    func=ACT.Identity,
+                    bias=bias_col[:, j : j + 1],
+                    scale=1.0,
+                )
+            biased[(block, g)] = with_bias
+
+        def turn_back(k):
+            block, tile_in_half = divmod(k, TILES)
+            nodes = slice(tile_in_half * P, (tile_in_half + 1) * P)
+            for g in range(3):
+                gate = GATE_ORDER[g]
+                adds_x = gate != C_GATE
+                bank = turned_pool.tile([P, HALF], F32, name="bank", tag="turned")
+                if adds_x:
+                    nc.tensor.matmul(
+                        out=bank[:],
+                        lhsT=ident_bf16[:],
+                        rhs=x_tiles[k][:, gate, :],
+                        start=True,
+                        stop=False,
+                    )
+                for ct in range(TILES):
+                    nc.tensor.matmul(
+                        out=bank[:, ct * P : (ct + 1) * P],
+                        lhsT=biased[(block, g)][:, ct, nodes],
+                        rhs=ident_f32[:],
+                        is_transpose=True,
+                        start=not adds_x,
+                        stop=(not adds_x) or ct == TILES - 1,
+                    )
+                turned[(k, gate)] = bank
+
+        def sigmoids(k):
+            reset = gate_pool.tile([P, HALF], F32, name="reset", tag="reset")
+            nc.scalar.activation(out=reset[:], in_=turned[(k, R_GATE)][:], func=ACT.Sigmoid)
+            reset_tiles[k] = reset
+            update = gate_pool.tile([P, HALF], F32, name="update", tag="update")
+            nc.scalar.activation(out=update[:], in_=turned[(k, Z_GATE)][:], func=ACT.Sigmoid)
+            update_tiles[k] = update
+
+        def h_block(k):
+            block, tile_in_half = divmod(k, TILES)
+            col_half, node_half = divmod(block, 2)
+            node_tile = node_half * TILES + tile_in_half
+            return node_tile, slice(col_half * HALF, (col_half + 1) * HALF)
+
+        for it in range(FIRST_ITERATION, STEPS + 1):
+            this_step = 0 <= it < STEPS
+            last_step = 0 <= it - 1 < STEPS
+            next_step = 0 <= it + 1 < STEPS
+
+            col_half, g = divmod(it + 5 + LOAD_AHEAD, 8)
+            if 0 <= col_half < 2 and g < 3:
+                load_w(col_half, g)
+            if 0 <= it + 1 + LOAD_AHEAD < STEPS:
+                load_x(it + 1 + LOAD_AHEAD)
+            node_half, rest = divmod(it + 5 + LOAD_AHEAD, 4)
+            if 0 <= node_half < 2 and rest == 0:
+                load_h(node_half)
+
+            if this_step:
+                cand = reset_tiles[it]
+                nc.vector.tensor_mul(out=cand[:], in0=turned[(it, C_GATE)][:], in1=cand[:])
+            if last_step:
+                node_tile, cols = h_block(it - 1)
+                mix = mix_pool.tile([P, HALF], F32, name="mix", tag="mix")
+                mix_tiles[it - 1] = mix
+                nc.vector.tensor_sub(
+                    out=mix[:], in0=h_sb[:, node_tile, cols], in1=reset_tiles[it - 1][:]
+                )
+            if this_step:
+                nc.vector.tensor_add(out=cand[:], in0=cand[:], in1=x_tiles[it][:, C_GATE, :])
+
+            block, g = divmod(it + 3, 4)
+            if 0 <= block < BLOCKS and g < 3:
+                add_bias(block, g)
+            if this_step:
+                nc.scalar.activation(out=cand[:], in_=cand[:], func=ACT.Tanh)
+            if next_step:
+                turn_back(it + 1)
+                sigmoids(it + 1)
+
+            if last_step:
+                nc.vector.tensor_mul(out=mix[:], in0=mix[:], in1=update_tiles[it - 1][:])
+
+            node_half, rest = divmod(it + 4, 4)
+            if 0 <= node_half < 2 and rest == 0:
+                quantise_h(node_half)
+            col_half, g = divmod(it + 5, 8)
+            if 0 <= col_half < 2 and g < 3:
+                prepare_w(col_half, g)
+            node_half, rest = divmod(it + 5, 4)
+            if 0 <= node_half < 2 and rest == 0:
+                transpose_h(node_half)
+
+            if last_step:
+                nc.vector.tensor_add(out=mix[:], in0=mix[:], in1=reset_tiles[it - 1][:])
+                nc.sync.dma_start(
+                    out=out_rows[node_tile * P : (node_tile + 1) * P, cols], in_=mix[:]
+                )
+
+            block, g = divmod(it + 4, 4)
+            if 0 <= block < BLOCKS and g < 3:
+                multiply_gate(block, g)

@@ -26,8 +26,12 @@ GATE_ORDER = (R_GATE, C_GATE, Z_GATE)
 
 FLOPS = 2 * NODES * C * 3 * C
 
-LOAD_AHEAD = 4
-FIRST_ITERATION = -5 - LOAD_AHEAD
+GROUPS_PER_PIECE = 3
+PIECES = 3 * BLOCKS * TILES // GROUPS_PER_PIECE
+MX_AHEAD = 6
+MIX_LAG = 2
+X_AHEAD = 6
+FIRST_ITERATION = -7
 
 
 def tile_gatedgraphconvolution_pb_kernel(
@@ -43,9 +47,10 @@ def tile_gatedgraphconvolution_pb_kernel(
         keep = ctx.enter_context(tc.tile_pool(name="keep", bufs=1))
         w_raw_pool = ctx.enter_context(tc.tile_pool(name="w_raw", bufs=6))
         w_grouped_pool = ctx.enter_context(tc.tile_pool(name="w_grouped", bufs=4))
-        x_pool = ctx.enter_context(tc.tile_pool(name="x", bufs=6))
+        x_pool = ctx.enter_context(tc.tile_pool(name="x", bufs=X_AHEAD + 2))
         biased_pool = ctx.enter_context(tc.tile_pool(name="biased", bufs=2))
-        gate_pool = ctx.enter_context(tc.tile_pool(name="gates", bufs=3))
+        reset_pool = ctx.enter_context(tc.tile_pool(name="reset", bufs=MIX_LAG + 3))
+        update_pool = ctx.enter_context(tc.tile_pool(name="update", bufs=MIX_LAG + 2))
         mix_pool = ctx.enter_context(tc.tile_pool(name="mix", bufs=4))
         product_pool = ctx.enter_context(tc.psum_pool(name="product", bufs=4))
         turned_pool = ctx.enter_context(tc.psum_pool(name="turned", bufs=4))
@@ -86,13 +91,13 @@ def tile_gatedgraphconvolution_pb_kernel(
             return (col_half * 3 + g) * PASSES + s
 
         w_raw = {}
+        w_grouped = {}
         x_tiles = {}
         products = {}
         biased = {}
         turned = {}
         reset_tiles = {}
         update_tiles = {}
-        mix_tiles = {}
 
         def load_w(col_half, g):
             col0 = GATE_ORDER[g] * C + col_half * HALF
@@ -109,38 +114,44 @@ def tile_gatedgraphconvolution_pb_kernel(
                 in_=rows.rearrange("(t p) c -> p t c", p=P),
             )
 
-        def load_x(k):
+        def place(k):
             block, tile_in_half = divmod(k, TILES)
             col_half, node_half = divmod(block, 2)
-            row0 = (node_half * TILES + tile_in_half) * P
+            return node_half * TILES + tile_in_half, slice(col_half * HALF, (col_half + 1) * HALF)
+
+        def load_x(k):
+            node_tile, cols = place(k)
             x_t = x_pool.tile([P, 3, HALF], BF16, name="x_t", tag="x_t")
-            cols = x_proj[row0 : row0 + P, :].rearrange("p (g c) -> p g c", g=3)
-            nc.sync.dma_start(out=x_t[:], in_=cols[:, :, col_half * HALF : (col_half + 1) * HALF])
+            rows = x_proj[node_tile * P : (node_tile + 1) * P, :]
+            nc.sync.dma_start(out=x_t[:], in_=rows.rearrange("p (g c) -> p g c", g=3)[:, :, cols])
             x_tiles[k] = x_t
 
-        def prepare_w(col_half, g):
-            grouped = []
+        def regroup_w(col_half, g):
             for s in range(PASSES):
-                w_grouped = w_grouped_pool.tile(
+                grouped = w_grouped_pool.tile(
                     [P, HALF, PACK], BF16, name="w_grouped", tag="w_grouped", align_bytes=64
                 )
                 nc.vector.tensor_copy(
-                    out=w_grouped[:].rearrange("p (c i) t -> p c t i", i=4),
+                    out=grouped[:].rearrange("p (c i) t -> p c t i", i=4),
                     in_=w_raw[(col_half, g, s)][:].rearrange("p t (c i) -> p c t i", i=4),
                 )
-                grouped.append(w_grouped)
+                w_grouped[(col_half, g, s)] = grouped
+
+        def quantise_w(col_half, g):
             for s in range(PASSES):
                 chunk = w_chunk(col_half, g, s)
                 nc.vector.quantize_mx(
                     out=w_codes[:, chunk, :].bitcast(FP8X4),
                     scales=w_scales[:, chunk, :],
-                    in_=grouped[s][:].rearrange("p c t -> p (c t)"),
+                    in_=w_grouped[(col_half, g, s)][:].rearrange("p c t -> p (c t)"),
                 )
 
         def transpose_h(node_half):
             for s in range(PASSES):
                 for pair in range(TILES // 2):
-                    h_turned = turned_pool.tile([P, 2, 2 * P], F32, name="h_turned", tag="turned")
+                    h_turned = product_pool.tile(
+                        [P, 2, 2 * P], F32, name="h_turned", tag="product"
+                    )
                     for j in range(2):
                         node_tile = node_half * TILES + 2 * pair + j
                         words = h_sb[:, node_tile, :].bitcast(F32).rearrange(
@@ -160,143 +171,153 @@ def tile_gatedgraphconvolution_pb_kernel(
 
         def quantise_h(node_half):
             nodes = slice(node_half * HALF, (node_half + 1) * HALF)
+            values = slice(node_half * HALF * PACK, (node_half + 1) * HALF * PACK)
             for s in range(PASSES):
                 nc.vector.quantize_mx(
                     out=h_codes[:, s, nodes].bitcast(FP8X4),
                     scales=h_scales[:, s, nodes],
-                    in_=h_grouped_values[:, s, node_half * HALF * PACK : (node_half + 1) * HALF * PACK],
+                    in_=h_grouped_values[:, s, values],
                 )
 
-        def multiply_gate(block, g):
+        def groups_of_piece(piece):
+            if not 0 <= piece < PIECES:
+                return []
+            first = piece * GROUPS_PER_PIECE
+            return [
+                (q // (3 * TILES), q % (3 * TILES) // TILES, q % TILES)
+                for q in range(first, first + GROUPS_PER_PIECE)
+            ]
+
+        def multiply(block, g, ct):
             col_half, node_half = divmod(block, 2)
             nodes = slice(node_half * HALF, (node_half + 1) * HALF)
-            for ct in range(TILES):
-                cols = slice(ct * P, (ct + 1) * P)
-                product = product_pool.tile([P, HALF], F32, name="product", tag="product")
-                for s in range(PASSES):
-                    chunk = w_chunk(col_half, g, s)
-                    nc.tensor.matmul_mx(
-                        out=product[:],
-                        lhsT=w_codes[:, chunk, cols].bitcast(FP8X4),
-                        lhsT_scale=w_scales[:, chunk, cols],
-                        rhs=h_codes[:, s, nodes].bitcast(FP8X4),
-                        rhs_scale=h_scales[:, s, nodes],
-                        start=(s == 0),
-                        stop=(s == PASSES - 1),
-                    )
-                products[(block, g, ct)] = product
-
-        def add_bias(block, g):
-            col_half = block // 2
-            with_bias = biased_pool.tile(
-                [P, TILES, HALF], F32, name="with_bias", tag="with_bias_%d" % g
-            )
-            for ct in range(TILES):
-                j = GATE_ORDER[g] * (C // P) + col_half * TILES + ct
-                nc.scalar.activation(
-                    out=with_bias[:, ct, :],
-                    in_=products[(block, g, ct)][:],
-                    func=ACT.Identity,
-                    bias=bias_col[:, j : j + 1],
-                    scale=1.0,
+            cols = slice(ct * P, (ct + 1) * P)
+            product = product_pool.tile([P, HALF], F32, name="product", tag="product")
+            for s in range(PASSES):
+                chunk = w_chunk(col_half, g, s)
+                nc.tensor.matmul_mx(
+                    out=product[:],
+                    lhsT=w_codes[:, chunk, cols].bitcast(FP8X4),
+                    lhsT_scale=w_scales[:, chunk, cols],
+                    rhs=h_codes[:, s, nodes].bitcast(FP8X4),
+                    rhs_scale=h_scales[:, s, nodes],
+                    start=(s == 0),
+                    stop=(s == PASSES - 1),
                 )
-            biased[(block, g)] = with_bias
+            products[(block, g, ct)] = product
 
-        def turn_back(k):
+        def add_bias(block, g, ct):
+            if ct == 0:
+                biased[(block, g)] = biased_pool.tile(
+                    [P, TILES, HALF], F32, name="with_bias", tag="with_bias_%d" % g
+                )
+            j = GATE_ORDER[g] * (C // P) + (block // 2) * TILES + ct
+            nc.scalar.activation(
+                out=biased[(block, g)][:, ct, :],
+                in_=products[(block, g, ct)][:],
+                func=ACT.Identity,
+                bias=bias_col[:, j : j + 1],
+                scale=1.0,
+            )
+
+        def turn_back(k, gate):
             block, tile_in_half = divmod(k, TILES)
             nodes = slice(tile_in_half * P, (tile_in_half + 1) * P)
-            for g in range(3):
-                gate = GATE_ORDER[g]
-                adds_x = gate != C_GATE
-                bank = turned_pool.tile([P, HALF], F32, name="bank", tag="turned")
-                if adds_x:
-                    nc.tensor.matmul(
-                        out=bank[:],
-                        lhsT=ident_bf16[:],
-                        rhs=x_tiles[k][:, gate, :],
-                        start=True,
-                        stop=False,
-                    )
-                for ct in range(TILES):
-                    nc.tensor.matmul(
-                        out=bank[:, ct * P : (ct + 1) * P],
-                        lhsT=biased[(block, g)][:, ct, nodes],
-                        rhs=ident_f32[:],
-                        is_transpose=True,
-                        start=not adds_x,
-                        stop=(not adds_x) or ct == TILES - 1,
-                    )
-                turned[(k, gate)] = bank
-
-        def sigmoids(k):
-            reset = gate_pool.tile([P, HALF], F32, name="reset", tag="reset")
-            nc.scalar.activation(out=reset[:], in_=turned[(k, R_GATE)][:], func=ACT.Sigmoid)
-            reset_tiles[k] = reset
-            update = gate_pool.tile([P, HALF], F32, name="update", tag="update")
-            nc.scalar.activation(out=update[:], in_=turned[(k, Z_GATE)][:], func=ACT.Sigmoid)
-            update_tiles[k] = update
-
-        def h_block(k):
-            block, tile_in_half = divmod(k, TILES)
-            col_half, node_half = divmod(block, 2)
-            node_tile = node_half * TILES + tile_in_half
-            return node_tile, slice(col_half * HALF, (col_half + 1) * HALF)
-
-        for it in range(FIRST_ITERATION, STEPS + 1):
-            this_step = 0 <= it < STEPS
-            last_step = 0 <= it - 1 < STEPS
-            next_step = 0 <= it + 1 < STEPS
-
-            col_half, g = divmod(it + 5 + LOAD_AHEAD, 8)
-            if 0 <= col_half < 2 and g < 3:
-                load_w(col_half, g)
-            if 0 <= it + 1 + LOAD_AHEAD < STEPS:
-                load_x(it + 1 + LOAD_AHEAD)
-            node_half, rest = divmod(it + 5 + LOAD_AHEAD, 4)
-            if 0 <= node_half < 2 and rest == 0:
-                load_h(node_half)
-
-            if this_step:
-                cand = reset_tiles[it]
-                nc.vector.tensor_mul(out=cand[:], in0=turned[(it, C_GATE)][:], in1=cand[:])
-            if last_step:
-                node_tile, cols = h_block(it - 1)
-                mix = mix_pool.tile([P, HALF], F32, name="mix", tag="mix")
-                mix_tiles[it - 1] = mix
-                nc.vector.tensor_sub(
-                    out=mix[:], in0=h_sb[:, node_tile, cols], in1=reset_tiles[it - 1][:]
+            adds_x = gate != C_GATE
+            bank = turned_pool.tile([P, HALF], F32, name="bank", tag="turned")
+            if adds_x:
+                nc.tensor.matmul(
+                    out=bank[:],
+                    lhsT=ident_bf16[:],
+                    rhs=x_tiles[k][:, gate, :],
+                    start=True,
+                    stop=False,
                 )
-            if this_step:
-                nc.vector.tensor_add(out=cand[:], in0=cand[:], in1=x_tiles[it][:, C_GATE, :])
+            for ct in range(TILES):
+                nc.tensor.matmul(
+                    out=bank[:, ct * P : (ct + 1) * P],
+                    lhsT=biased[(block, GATE_ORDER.index(gate))][:, ct, nodes],
+                    rhs=ident_f32[:],
+                    is_transpose=True,
+                    start=not adds_x,
+                    stop=(not adds_x) or ct == TILES - 1,
+                )
+            turned[(k, gate)] = bank
 
-            block, g = divmod(it + 3, 4)
-            if 0 <= block < BLOCKS and g < 3:
-                add_bias(block, g)
-            if this_step:
+        def sigmoid(k, gate, pool, tiles):
+            tiles[k] = pool.tile([P, HALF], F32, name="gate_%d" % gate, tag="gate_%d" % gate)
+            nc.scalar.activation(out=tiles[k][:], in_=turned[(k, gate)][:], func=ACT.Sigmoid)
+
+        def is_step(k):
+            return 0 <= k < STEPS
+
+        load_w(0, 0)
+        load_h(0)
+        load_w(0, 1)
+        load_w(0, 2)
+        load_x(0)
+        load_h(1)
+        for g in range(3):
+            load_w(1, g)
+            load_x(1 + g)
+        for k in range(4, X_AHEAD):
+            load_x(k)
+
+        for it in range(FIRST_ITERATION, STEPS + MIX_LAG):
+            mixed = it - MIX_LAG
+            if it >= 0 and is_step(it + X_AHEAD):
+                load_x(it + X_AHEAD)
+
+            if is_step(it - 1):
+                cand = reset_tiles[it - 1]
                 nc.scalar.activation(out=cand[:], in_=cand[:], func=ACT.Tanh)
-            if next_step:
-                turn_back(it + 1)
-                sigmoids(it + 1)
+            if is_step(it + 1):
+                sigmoid(it + 1, R_GATE, reset_pool, reset_tiles)
+            if is_step(it):
+                sigmoid(it, Z_GATE, update_pool, update_tiles)
 
-            if last_step:
-                nc.vector.tensor_mul(out=mix[:], in0=mix[:], in1=update_tiles[it - 1][:])
+            if is_step(it):
+                nc.vector.tensor_mul(
+                    out=reset_tiles[it][:], in0=turned[(it, C_GATE)][:], in1=reset_tiles[it][:]
+                )
+            if is_step(mixed):
+                node_tile, cols = place(mixed)
+                mix = mix_pool.tile([P, HALF], F32, name="mix", tag="mix")
+                nc.vector.tensor_sub(
+                    out=mix[:], in0=h_sb[:, node_tile, cols], in1=reset_tiles[mixed][:]
+                )
+            if is_step(it):
+                nc.vector.tensor_add(
+                    out=reset_tiles[it][:], in0=reset_tiles[it][:], in1=x_tiles[it][:, C_GATE, :]
+                )
+            if is_step(mixed):
+                nc.vector.tensor_mul(out=mix[:], in0=mix[:], in1=update_tiles[mixed][:])
 
-            node_half, rest = divmod(it + 4, 4)
+            for block, g, ct in groups_of_piece(it + MX_AHEAD - 1):
+                add_bias(block, g, ct)
+
+            col_half, g = divmod(it - FIRST_ITERATION, 3)
+            if col_half < 2:
+                regroup_w(col_half, g)
+            node_half, rest = divmod(it - FIRST_ITERATION - 1, 3)
             if 0 <= node_half < 2 and rest == 0:
                 quantise_h(node_half)
-            col_half, g = divmod(it + 5, 8)
-            if 0 <= col_half < 2 and g < 3:
-                prepare_w(col_half, g)
-            node_half, rest = divmod(it + 5, 4)
-            if 0 <= node_half < 2 and rest == 0:
-                transpose_h(node_half)
+            if col_half < 2:
+                quantise_w(col_half, g)
 
-            if last_step:
-                nc.vector.tensor_add(out=mix[:], in0=mix[:], in1=reset_tiles[it - 1][:])
+            if is_step(mixed):
+                nc.vector.tensor_add(out=mix[:], in0=mix[:], in1=reset_tiles[mixed][:])
                 nc.sync.dma_start(
                     out=out_rows[node_tile * P : (node_tile + 1) * P, cols], in_=mix[:]
                 )
 
-            block, g = divmod(it + 4, 4)
-            if 0 <= block < BLOCKS and g < 3:
-                multiply_gate(block, g)
+            if is_step(it + 1):
+                turn_back(it + 1, C_GATE)
+                turn_back(it + 1, Z_GATE)
+            if is_step(it + 2):
+                turn_back(it + 2, R_GATE)
+            node_half, rest = divmod(it - FIRST_ITERATION, 3)
+            if node_half < 2 and rest == 0:
+                transpose_h(node_half)
+            for block, g, ct in groups_of_piece(it + MX_AHEAD):
+                multiply(block, g, ct)

@@ -42,7 +42,6 @@ def tile_gatedgraphconvolution_pb_kernel(
     out_rows = out.flatten_outer_dims()
 
     with ExitStack() as ctx:
-        ctx.enter_context(tc.manual_schedule())
         const = ctx.enter_context(tc.tile_pool(name="const", bufs=1))
         keep = ctx.enter_context(tc.tile_pool(name="keep", bufs=1))
         w_raw_pool = ctx.enter_context(tc.tile_pool(name="w_raw", bufs=6))

@@ -9,6 +9,7 @@ U32 = mybir.dt.uint32
 U8 = mybir.dt.uint8
 FP8X4 = mybir.dt.float8_e4m3fn_x4
 ACT = mybir.ActivationFunctionType
+ALU = mybir.AluOpType
 
 P = 128
 PACK = 4
@@ -19,19 +20,26 @@ PASSES = C // K_PASS
 HALF = 512
 TILES = HALF // P
 BLOCKS = 4
-STEPS = BLOCKS * TILES
+ITEMS = BLOCKS * TILES
 
 Z_GATE, R_GATE, C_GATE = 0, 1, 2
-GATE_ORDER = (R_GATE, C_GATE, Z_GATE)
 
 FLOPS = 2 * NODES * C * 3 * C
 
-GROUPS_PER_PIECE = 3
-PIECES = 3 * BLOCKS * TILES // GROUPS_PER_PIECE
-MX_AHEAD = 6
-MIX_LAG = 2
-X_AHEAD = 6
-FIRST_ITERATION = -7
+R_TURN_LAG = 4
+C_MX_LAG = 5
+C_MUL_LAG = 5
+C_TURN_LAG = 9
+Z_MX_LAG = 1
+Z_TURN_LAG = Z_MX_LAG + 4
+MIX_LAG = 10
+
+ON_SCALAR = (
+    (0, Z_GATE, 0), (0, Z_GATE, 1), (0, C_GATE, 0), (0, C_GATE, 1),
+    (1, Z_GATE, 0), (1, C_GATE, 0), (1, C_GATE, 1),
+)
+W_PREP = {0: (0, Z_GATE), 2: (0, C_GATE), 4: (1, R_GATE), 6: (1, Z_GATE), 8: (1, C_GATE)}
+H_PREP = {1: 1}
 
 
 def tile_gatedgraphconvolution_pb_kernel(
@@ -45,14 +53,18 @@ def tile_gatedgraphconvolution_pb_kernel(
         const = ctx.enter_context(tc.tile_pool(name="const", bufs=1))
         keep = ctx.enter_context(tc.tile_pool(name="keep", bufs=1))
         w_raw_pool = ctx.enter_context(tc.tile_pool(name="w_raw", bufs=6))
-        w_grouped_pool = ctx.enter_context(tc.tile_pool(name="w_grouped", bufs=4))
-        x_pool = ctx.enter_context(tc.tile_pool(name="x", bufs=X_AHEAD + 2))
-        biased_pool = ctx.enter_context(tc.tile_pool(name="biased", bufs=2))
-        reset_pool = ctx.enter_context(tc.tile_pool(name="reset", bufs=MIX_LAG + 3))
-        update_pool = ctx.enter_context(tc.tile_pool(name="update", bufs=MIX_LAG + 2))
+        grouped_pool = ctx.enter_context(tc.tile_pool(name="grouped", bufs=5))
+        x_pool = ctx.enter_context(tc.tile_pool(name="x", bufs=ITEMS))
+        ar_pool = ctx.enter_context(tc.tile_pool(name="ar", bufs=8))
+        rt_pool = ctx.enter_context(tc.tile_pool(name="rt", bufs=3))
+        mt_pool = ctx.enter_context(tc.tile_pool(name="mt", bufs=8))
+        zb_pool = ctx.enter_context(tc.tile_pool(name="zb", bufs=8))
+        cand_pool = ctx.enter_context(tc.tile_pool(name="cand", bufs=3))
+        z_pool = ctx.enter_context(tc.tile_pool(name="z", bufs=7))
         mix_pool = ctx.enter_context(tc.tile_pool(name="mix", bufs=4))
-        product_pool = ctx.enter_context(tc.psum_pool(name="product", bufs=4))
-        turned_pool = ctx.enter_context(tc.psum_pool(name="turned", bufs=4))
+        prod_n = ctx.enter_context(tc.psum_pool(name="prod_n", bufs=2))
+        prod_t = ctx.enter_context(tc.psum_pool(name="prod_t", bufs=3))
+        turned_pool = ctx.enter_context(tc.psum_pool(name="turned", bufs=3))
 
         ident_f32 = const.tile([P, P], F32, name="ident_f32")
         make_identity(nc, ident_f32[:])
@@ -75,85 +87,92 @@ def tile_gatedgraphconvolution_pb_kernel(
         nc.vector.tensor_copy(out=bias_col[:], in_=bias_turned[:, 0:bias_tiles])
 
         h_sb = keep.tile([P, NODES // P, C], BF16, name="h_sb")
-        h_grouped = keep.tile([P, PASSES * NODES * PACK], BF16, name="h_grouped", align_bytes=64)
-        h_grouped_words = h_grouped[:].bitcast(F32).rearrange(
-            "p (s n u) -> p s n u", s=PASSES, u=2
-        )
-        h_grouped_values = h_grouped[:].rearrange("p (s m) -> p s m", s=PASSES)
         h_codes = keep.tile([P, PASSES, NODES], U32, name="h_codes", align_bytes=64)
         h_scales = keep.tile([P, PASSES, NODES], U8, name="h_scales", align_bytes=64)
         w_chunks = 2 * 3 * PASSES
         w_codes = keep.tile([P, w_chunks, HALF], U32, name="w_codes", align_bytes=64)
         w_scales = keep.tile([P, w_chunks, HALF], U8, name="w_scales", align_bytes=64)
 
-        def w_chunk(col_half, g, s):
-            return (col_half * 3 + g) * PASSES + s
+        def w_chunk(cb, gate, s):
+            return (cb * 3 + gate) * PASSES + s
 
         w_raw = {}
-        w_grouped = {}
         x_tiles = {}
-        products = {}
-        biased = {}
-        turned = {}
-        reset_tiles = {}
-        update_tiles = {}
+        ar = {}
+        rt = {}
+        c_prod = {}
+        mt = {}
+        zb = {}
+        cand = {}
+        z_tiles = {}
 
-        def load_w(col_half, g):
-            col0 = GATE_ORDER[g] * C + col_half * HALF
+        def split(i):
+            b, q = divmod(i, TILES)
+            cb, nb = divmod(b, 2)
+            return b, q, cb, nb
+
+        def is_item(i):
+            return 0 <= i < ITEMS
+
+        def load_w(cb, gate):
+            col0 = gate * C + cb * HALF
             for s in range(PASSES):
                 raw = w_raw_pool.tile([P, PACK, HALF], BF16, name="w_raw", tag="w_raw")
                 rows = recurrent_kernel[s * K_PASS : (s + 1) * K_PASS, col0 : col0 + HALF]
                 nc.sync.dma_start(out=raw[:], in_=rows.rearrange("(p t) c -> p t c", t=PACK))
-                w_raw[(col_half, g, s)] = raw
+                w_raw[(cb, gate, s)] = raw
 
-        def load_h(node_half):
-            rows = h_rows[node_half * HALF : (node_half + 1) * HALF, :]
+        def load_h(nb):
+            rows = h_rows[nb * HALF : (nb + 1) * HALF, :]
             nc.sync.dma_start(
-                out=h_sb[:, node_half * TILES : (node_half + 1) * TILES, :],
+                out=h_sb[:, nb * TILES : (nb + 1) * TILES, :],
                 in_=rows.rearrange("(t p) c -> p t c", p=P),
             )
 
-        def place(k):
-            block, tile_in_half = divmod(k, TILES)
-            col_half, node_half = divmod(block, 2)
-            return node_half * TILES + tile_in_half, slice(col_half * HALF, (col_half + 1) * HALF)
-
-        def load_x(k):
-            node_tile, cols = place(k)
+        def load_x(i):
+            b, q, cb, nb = split(i)
+            nt = nb * TILES + q
             x_t = x_pool.tile([P, 3, HALF], BF16, name="x_t", tag="x_t")
-            rows = x_proj[node_tile * P : (node_tile + 1) * P, :]
-            nc.sync.dma_start(out=x_t[:], in_=rows.rearrange("p (g c) -> p g c", g=3)[:, :, cols])
-            x_tiles[k] = x_t
+            rows = x_proj[nt * P : (nt + 1) * P, :]
+            nc.sync.dma_start(
+                out=x_t[:],
+                in_=rows.rearrange("p (g c) -> p g c", g=3)[:, :, cb * HALF : (cb + 1) * HALF],
+            )
+            x_tiles[i] = x_t
 
-        def regroup_w(col_half, g):
+        def prep_w(cb, gate):
+            grouped = {}
             for s in range(PASSES):
-                grouped = w_grouped_pool.tile(
-                    [P, HALF, PACK], BF16, name="w_grouped", tag="w_grouped", align_bytes=64
+                g_t = grouped_pool.tile(
+                    [P, HALF * PACK], BF16, name="grouped", tag="grouped", align_bytes=64
                 )
-                nc.vector.tensor_copy(
-                    out=grouped[:].rearrange("p (c i) t -> p c t i", i=4),
-                    in_=w_raw[(col_half, g, s)][:].rearrange("p t (c i) -> p c t i", i=4),
-                )
-                w_grouped[(col_half, g, s)] = grouped
-
-        def quantise_w(col_half, g):
+                dst = g_t[:].rearrange("p (c i t) -> p c t i", i=4, t=PACK)
+                src = w_raw[(cb, gate, s)][:].rearrange("p t (c i) -> p c t i", i=4)
+                if (cb, gate, s) in ON_SCALAR:
+                    nc.scalar.copy(out=dst, in_=src)
+                else:
+                    nc.vector.tensor_copy(out=dst, in_=src)
+                grouped[s] = g_t
             for s in range(PASSES):
-                chunk = w_chunk(col_half, g, s)
+                chunk = w_chunk(cb, gate, s)
                 nc.vector.quantize_mx(
                     out=w_codes[:, chunk, :].bitcast(FP8X4),
                     scales=w_scales[:, chunk, :],
-                    in_=w_grouped[(col_half, g, s)][:].rearrange("p c t -> p (c t)"),
+                    in_=grouped[s][:],
                 )
 
-        def transpose_h(node_half):
+        def prep_h(nb):
+            grouped = {}
             for s in range(PASSES):
+                g_t = grouped_pool.tile(
+                    [P, HALF * PACK], BF16, name="grouped", tag="grouped", align_bytes=64
+                )
+                g_words = g_t[:].bitcast(F32).rearrange("p (n u) -> p n u", u=2)
                 for pair in range(TILES // 2):
-                    h_turned = product_pool.tile(
-                        [P, 2, 2 * P], F32, name="h_turned", tag="product"
-                    )
+                    h_turned = prod_t.tile([P, 2, 2 * P], F32, name="h_turned", tag="prod_t")
                     for j in range(2):
-                        node_tile = node_half * TILES + 2 * pair + j
-                        words = h_sb[:, node_tile, :].bitcast(F32).rearrange(
+                        nt = nb * TILES + 2 * pair + j
+                        words = h_sb[:, nt, :].bitcast(F32).rearrange(
                             "p (s w u) -> p s u w", s=PASSES, u=2
                         )
                         for u in range(2):
@@ -162,40 +181,41 @@ def tile_gatedgraphconvolution_pb_kernel(
                                 in_=words[:, s, u, :],
                                 identity=ident_f32[:],
                             )
-                    node0 = node_half * HALF + pair * 2 * P
+                    n0 = pair * 2 * P
                     nc.scalar.copy(
-                        out=h_grouped_words[:, s, node0 : node0 + 2 * P, :],
+                        out=g_words[:, n0 : n0 + 2 * P, :],
                         in_=h_turned[:].rearrange("p u n -> p n u"),
                     )
-
-        def quantise_h(node_half):
-            nodes = slice(node_half * HALF, (node_half + 1) * HALF)
-            values = slice(node_half * HALF * PACK, (node_half + 1) * HALF * PACK)
+                grouped[s] = g_t
+            nodes = slice(nb * HALF, (nb + 1) * HALF)
             for s in range(PASSES):
                 nc.vector.quantize_mx(
                     out=h_codes[:, s, nodes].bitcast(FP8X4),
                     scales=h_scales[:, s, nodes],
-                    in_=h_grouped_values[:, s, values],
+                    in_=grouped[s][:],
                 )
 
-        def groups_of_piece(piece):
-            if not 0 <= piece < PIECES:
-                return []
-            first = piece * GROUPS_PER_PIECE
-            return [
-                (q // (3 * TILES), q % (3 * TILES) // TILES, q % TILES)
-                for q in range(first, first + GROUPS_PER_PIECE)
-            ]
-
-        def multiply(block, g, ct):
-            col_half, node_half = divmod(block, 2)
-            nodes = slice(node_half * HALF, (node_half + 1) * HALF)
-            cols = slice(ct * P, (ct + 1) * P)
-            product = product_pool.tile([P, HALF], F32, name="product", tag="product")
+        def mx_nodes_out(bank, cb, gate, nt):
+            nodes = slice(nt * P, (nt + 1) * P)
             for s in range(PASSES):
-                chunk = w_chunk(col_half, g, s)
+                chunk = w_chunk(cb, gate, s)
                 nc.tensor.matmul_mx(
-                    out=product[:],
+                    out=bank[:],
+                    lhsT=h_codes[:, s, nodes].bitcast(FP8X4),
+                    lhsT_scale=h_scales[:, s, nodes],
+                    rhs=w_codes[:, chunk, :].bitcast(FP8X4),
+                    rhs_scale=w_scales[:, chunk, :],
+                    start=(s == 0),
+                    stop=(s == PASSES - 1),
+                )
+
+        def mx_cols_out(bank, cb, gate, ct, nb):
+            nodes = slice(nb * HALF, (nb + 1) * HALF)
+            cols = slice(ct * P, (ct + 1) * P)
+            for s in range(PASSES):
+                chunk = w_chunk(cb, gate, s)
+                nc.tensor.matmul_mx(
+                    out=bank[:],
                     lhsT=w_codes[:, chunk, cols].bitcast(FP8X4),
                     lhsT_scale=w_scales[:, chunk, cols],
                     rhs=h_codes[:, s, nodes].bitcast(FP8X4),
@@ -203,120 +223,130 @@ def tile_gatedgraphconvolution_pb_kernel(
                     start=(s == 0),
                     stop=(s == PASSES - 1),
                 )
-            products[(block, g, ct)] = product
 
-        def add_bias(block, g, ct):
-            if ct == 0:
-                biased[(block, g)] = biased_pool.tile(
-                    [P, TILES, HALF], F32, name="with_bias", tag="with_bias_%d" % g
-                )
-            j = GATE_ORDER[g] * (C // P) + (block // 2) * TILES + ct
-            nc.scalar.activation(
-                out=biased[(block, g)][:, ct, :],
-                in_=products[(block, g, ct)][:],
-                func=ACT.Identity,
-                bias=bias_col[:, j : j + 1],
-                scale=1.0,
-            )
+        def bias_of(gate, cb, ct):
+            j = gate * (C // P) + cb * TILES + ct
+            return bias_col[:, j : j + 1]
 
-        def turn_back(k, gate):
-            block, tile_in_half = divmod(k, TILES)
-            nodes = slice(tile_in_half * P, (tile_in_half + 1) * P)
-            adds_x = gate != C_GATE
-            bank = turned_pool.tile([P, HALF], F32, name="bank", tag="turned")
+        def turn(bank, tiles, b, q, x_block):
+            adds_x = x_block is not None
             if adds_x:
                 nc.tensor.matmul(
-                    out=bank[:],
-                    lhsT=ident_bf16[:],
-                    rhs=x_tiles[k][:, gate, :],
-                    start=True,
-                    stop=False,
+                    out=bank[:], lhsT=ident_bf16[:], rhs=x_block, start=True, stop=False
                 )
-            for ct in range(TILES):
+            for t in range(TILES):
                 nc.tensor.matmul(
-                    out=bank[:, ct * P : (ct + 1) * P],
-                    lhsT=biased[(block, GATE_ORDER.index(gate))][:, ct, nodes],
+                    out=bank[:, t * P : (t + 1) * P],
+                    lhsT=tiles[(b, t)][:, q * P : (q + 1) * P],
                     rhs=ident_f32[:],
                     is_transpose=True,
                     start=not adds_x,
-                    stop=(not adds_x) or ct == TILES - 1,
+                    stop=(not adds_x) or t == TILES - 1,
                 )
-            turned[(k, gate)] = bank
 
-        def sigmoid(k, gate, pool, tiles):
-            tiles[k] = pool.tile([P, HALF], F32, name="gate_%d" % gate, tag="gate_%d" % gate)
-            nc.scalar.activation(out=tiles[k][:], in_=turned[(k, gate)][:], func=ACT.Sigmoid)
+        def r_product(i):
+            b, q, cb, nb = split(i)
+            bank = prod_n.tile([P, HALF], F32, name="r_prod", tag="prod_n")
+            mx_nodes_out(bank, cb, R_GATE, nb * TILES + q)
+            ar[(b, q)] = ar_pool.tile([P, HALF], F32, name="ar", tag="ar")
+            nc.vector.tensor_add(out=ar[(b, q)][:], in0=bank[:], in1=x_tiles[i][:, R_GATE, :])
 
-        def is_step(k):
-            return 0 <= k < STEPS
+        def r_turn(i):
+            b, q, cb, nb = split(i)
+            bank = turned_pool.tile([P, HALF], F32, name="r_bank", tag="turned")
+            turn(bank, ar, b, q, None)
+            rt[i] = rt_pool.tile([P, HALF], F32, name="rt", tag="rt")
+            nc.scalar.activation(
+                out=rt[i][:], in_=bank[:], func=ACT.Sigmoid, bias=bias_of(R_GATE, cb, q), scale=1.0
+            )
 
-        load_w(0, 0)
+        def c_product(i):
+            b, q, cb, nb = split(i)
+            c_prod[i] = prod_t.tile([P, HALF], F32, name="c_prod", tag="prod_t")
+            mx_cols_out(c_prod[i], cb, C_GATE, q, nb)
+
+        def c_multiply(i):
+            b, q, cb, nb = split(i)
+            mt[(b, q)] = mt_pool.tile([P, HALF], F32, name="mt", tag="mt")
+            nc.vector.scalar_tensor_tensor(
+                out=mt[(b, q)][:],
+                in0=c_prod[i][:],
+                scalar=bias_of(C_GATE, cb, q),
+                in1=rt[i][:],
+                op0=ALU.add,
+                op1=ALU.mult,
+            )
+
+        def c_turn(i):
+            b, q, cb, nb = split(i)
+            bank = turned_pool.tile([P, HALF], F32, name="c_bank", tag="turned")
+            turn(bank, mt, b, q, x_tiles[i][:, C_GATE, :])
+            cand[i] = cand_pool.tile([P, HALF], F32, name="cand", tag="cand")
+            nc.scalar.activation(out=cand[i][:], in_=bank[:], func=ACT.Tanh)
+
+        def z_product(i):
+            b, q, cb, nb = split(i)
+            bank = prod_t.tile([P, HALF], F32, name="z_prod", tag="prod_t")
+            mx_cols_out(bank, cb, Z_GATE, q, nb)
+            zb[(b, q)] = zb_pool.tile([P, HALF], F32, name="zb", tag="zb")
+            nc.scalar.activation(
+                out=zb[(b, q)][:], in_=bank[:], func=ACT.Identity,
+                bias=bias_of(Z_GATE, cb, q), scale=1.0,
+            )
+
+        def z_turn(i):
+            b, q, cb, nb = split(i)
+            bank = turned_pool.tile([P, HALF], F32, name="z_bank", tag="turned")
+            turn(bank, zb, b, q, x_tiles[i][:, Z_GATE, :])
+            z_tiles[i] = z_pool.tile([P, HALF], F32, name="z", tag="z")
+            nc.scalar.activation(out=z_tiles[i][:], in_=bank[:], func=ACT.Sigmoid)
+
+        def mix(i):
+            b, q, cb, nb = split(i)
+            nt = nb * TILES + q
+            cols = slice(cb * HALF, (cb + 1) * HALF)
+            m = mix_pool.tile([P, HALF], F32, name="mix", tag="mix")
+            nc.vector.tensor_sub(out=m[:], in0=h_sb[:, nt, cols], in1=cand[i][:])
+            nc.vector.tensor_mul(out=m[:], in0=m[:], in1=z_tiles[i][:])
+            nc.vector.tensor_add(out=m[:], in0=m[:], in1=cand[i][:])
+            nc.sync.dma_start(out=out_rows[nt * P : (nt + 1) * P, cols], in_=m[:])
+
+        load_w(0, R_GATE)
         load_h(0)
-        load_w(0, 1)
-        load_w(0, 2)
-        load_x(0)
+        for i in range(0, 4):
+            load_x(i)
+        load_w(0, Z_GATE)
+        load_w(0, C_GATE)
         load_h(1)
-        for g in range(3):
-            load_w(1, g)
-            load_x(1 + g)
-        for k in range(4, X_AHEAD):
-            load_x(k)
+        for i in range(4, 8):
+            load_x(i)
+        load_w(1, R_GATE)
+        load_w(1, Z_GATE)
+        load_w(1, C_GATE)
+        for i in range(8, ITEMS):
+            load_x(i)
 
-        for it in range(FIRST_ITERATION, STEPS + MIX_LAG):
-            mixed = it - MIX_LAG
-            if it >= 0 and is_step(it + X_AHEAD):
-                load_x(it + X_AHEAD)
+        prep_w(0, R_GATE)
+        prep_h(0)
 
-            if is_step(it - 1):
-                cand = reset_tiles[it - 1]
-                nc.scalar.activation(out=cand[:], in_=cand[:], func=ACT.Tanh)
-            if is_step(it + 1):
-                sigmoid(it + 1, R_GATE, reset_pool, reset_tiles)
-            if is_step(it):
-                sigmoid(it, Z_GATE, update_pool, update_tiles)
-
-            if is_step(it):
-                nc.vector.tensor_mul(
-                    out=reset_tiles[it][:], in0=turned[(it, C_GATE)][:], in1=reset_tiles[it][:]
-                )
-            if is_step(mixed):
-                node_tile, cols = place(mixed)
-                mix = mix_pool.tile([P, HALF], F32, name="mix", tag="mix")
-                nc.vector.tensor_sub(
-                    out=mix[:], in0=h_sb[:, node_tile, cols], in1=reset_tiles[mixed][:]
-                )
-            if is_step(it):
-                nc.vector.tensor_add(
-                    out=reset_tiles[it][:], in0=reset_tiles[it][:], in1=x_tiles[it][:, C_GATE, :]
-                )
-            if is_step(mixed):
-                nc.vector.tensor_mul(out=mix[:], in0=mix[:], in1=update_tiles[mixed][:])
-
-            for block, g, ct in groups_of_piece(it + MX_AHEAD - 1):
-                add_bias(block, g, ct)
-
-            col_half, g = divmod(it - FIRST_ITERATION, 3)
-            if col_half < 2:
-                regroup_w(col_half, g)
-            node_half, rest = divmod(it - FIRST_ITERATION - 1, 3)
-            if 0 <= node_half < 2 and rest == 0:
-                quantise_h(node_half)
-            if col_half < 2:
-                quantise_w(col_half, g)
-
-            if is_step(mixed):
-                nc.vector.tensor_add(out=mix[:], in0=mix[:], in1=reset_tiles[mixed][:])
-                nc.sync.dma_start(
-                    out=out_rows[node_tile * P : (node_tile + 1) * P, cols], in_=mix[:]
-                )
-
-            if is_step(it + 1):
-                turn_back(it + 1, C_GATE)
-                turn_back(it + 1, Z_GATE)
-            if is_step(it + 2):
-                turn_back(it + 2, R_GATE)
-            node_half, rest = divmod(it - FIRST_ITERATION, 3)
-            if node_half < 2 and rest == 0:
-                transpose_h(node_half)
-            for block, g, ct in groups_of_piece(it + MX_AHEAD):
-                multiply(block, g, ct)
+        for tick in range(ITEMS + MIX_LAG):
+            if is_item(tick - MIX_LAG):
+                mix(tick - MIX_LAG)
+            if is_item(tick - C_TURN_LAG):
+                c_turn(tick - C_TURN_LAG)
+            if is_item(tick - Z_TURN_LAG):
+                z_turn(tick - Z_TURN_LAG)
+            if is_item(tick - C_MX_LAG):
+                c_product(tick - C_MX_LAG)
+            if is_item(tick - C_MUL_LAG):
+                c_multiply(tick - C_MUL_LAG)
+            if is_item(tick - R_TURN_LAG):
+                r_turn(tick - R_TURN_LAG)
+            if is_item(tick - Z_MX_LAG):
+                z_product(tick - Z_MX_LAG)
+            if is_item(tick):
+                r_product(tick)
+            if tick in H_PREP:
+                prep_h(H_PREP[tick])
+            if tick in W_PREP:
+                prep_w(W_PREP[tick][0], W_PREP[tick][1])

@@ -26,19 +26,20 @@ Z_GATE, R_GATE, C_GATE = 0, 1, 2
 
 FLOPS = 2 * NODES * C * 3 * C
 
-R_TURN_LAG = 4
+R_ADD_LAG = 1
+R_TURN_LAG = 5
 C_MX_LAG = 5
-C_MUL_LAG = 5
-C_TURN_LAG = 9
-Z_MX_LAG = 1
-Z_TURN_LAG = Z_MX_LAG + 4
-MIX_LAG = 10
-
+C_MUL_LAG = 6
+C_TURN_LAG = 10
+Z_MX_LAG = 2
+Z_TURN_LAG = Z_MX_LAG + 5
+MIX_LAG = 11
+S_PIECES = 4
+PSUM_R, PSUM_C, PSUM_Z, PSUM_TURNED = 2, 2, 1, 3
 ON_SCALAR = (
-    (0, Z_GATE, 0), (0, Z_GATE, 1), (0, C_GATE, 0), (0, C_GATE, 1),
-    (1, Z_GATE, 0), (1, C_GATE, 0), (1, C_GATE, 1),
+    (0, Z_GATE, 1), (0, C_GATE, 1), (1, R_GATE, 1), (1, Z_GATE, 1), (1, C_GATE, 1),
 )
-W_PREP = {0: (0, Z_GATE), 2: (0, C_GATE), 4: (1, R_GATE), 6: (1, Z_GATE), 8: (1, C_GATE)}
+W_PREP = {0: (0, Z_GATE), 2: (0, C_GATE), 5: (1, R_GATE), 7: (1, Z_GATE), 9: (1, C_GATE)}
 H_PREP = {1: 1}
 
 
@@ -62,9 +63,10 @@ def tile_gatedgraphconvolution_pb_kernel(
         cand_pool = ctx.enter_context(tc.tile_pool(name="cand", bufs=3))
         z_pool = ctx.enter_context(tc.tile_pool(name="z", bufs=7))
         mix_pool = ctx.enter_context(tc.tile_pool(name="mix", bufs=4))
-        prod_n = ctx.enter_context(tc.psum_pool(name="prod_n", bufs=2))
-        prod_t = ctx.enter_context(tc.psum_pool(name="prod_t", bufs=3))
-        turned_pool = ctx.enter_context(tc.psum_pool(name="turned", bufs=3))
+        prod_n = ctx.enter_context(tc.psum_pool(name="prod_n", bufs=PSUM_R))
+        prod_t = ctx.enter_context(tc.psum_pool(name="prod_t", bufs=PSUM_Z))
+        prod_c = ctx.enter_context(tc.psum_pool(name="prod_c", bufs=PSUM_C))
+        turned_pool = ctx.enter_context(tc.psum_pool(name="turned", bufs=PSUM_TURNED))
 
         ident_f32 = const.tile([P, P], F32, name="ident_f32")
         make_identity(nc, ident_f32[:])
@@ -123,11 +125,12 @@ def tile_gatedgraphconvolution_pb_kernel(
                 w_raw[(cb, gate, s)] = raw
 
         def load_h(nb):
-            rows = h_rows[nb * HALF : (nb + 1) * HALF, :]
-            nc.sync.dma_start(
-                out=h_sb[:, nb * TILES : (nb + 1) * TILES, :],
-                in_=rows.rearrange("(t p) c -> p t c", p=P),
-            )
+            for half in range(2):
+                nt0 = nb * TILES + 2 * half
+                rows = h_rows[nt0 * P : (nt0 + 2) * P, :]
+                nc.sync.dma_start(
+                    out=h_sb[:, nt0 : nt0 + 2, :], in_=rows.rearrange("(t p) c -> p t c", p=P)
+                )
 
         def load_x(i):
             b, q, cb, nb = split(i)
@@ -140,8 +143,10 @@ def tile_gatedgraphconvolution_pb_kernel(
             )
             x_tiles[i] = x_t
 
-        def prep_w(cb, gate):
-            grouped = {}
+        grouped_w = {}
+        grouped_h = {}
+
+        def w_regroup(cb, gate):
             for s in range(PASSES):
                 g_t = grouped_pool.tile(
                     [P, HALF * PACK], BF16, name="grouped", tag="grouped", align_bytes=64
@@ -149,27 +154,32 @@ def tile_gatedgraphconvolution_pb_kernel(
                 dst = g_t[:].rearrange("p (c i t) -> p c t i", i=4, t=PACK)
                 src = w_raw[(cb, gate, s)][:].rearrange("p t (c i) -> p c t i", i=4)
                 if (cb, gate, s) in ON_SCALAR:
-                    nc.scalar.copy(out=dst, in_=src)
+                    step = HALF // 4 // S_PIECES
+                    for piece in range(S_PIECES):
+                        part = slice(piece * step, (piece + 1) * step)
+                        nc.scalar.copy(out=dst[:, part, :, :], in_=src[:, part, :, :])
                 else:
                     nc.vector.tensor_copy(out=dst, in_=src)
-                grouped[s] = g_t
+                grouped_w[(cb, gate, s)] = g_t
+
+        def w_quantise(cb, gate):
             for s in range(PASSES):
                 chunk = w_chunk(cb, gate, s)
                 nc.vector.quantize_mx(
                     out=w_codes[:, chunk, :].bitcast(FP8X4),
                     scales=w_scales[:, chunk, :],
-                    in_=grouped[s][:],
+                    in_=grouped_w[(cb, gate, s)][:],
                 )
 
-        def prep_h(nb):
-            grouped = {}
+        def h_transposes(nb):
             for s in range(PASSES):
-                g_t = grouped_pool.tile(
+                grouped_h[(nb, s)] = grouped_pool.tile(
                     [P, HALF * PACK], BF16, name="grouped", tag="grouped", align_bytes=64
                 )
-                g_words = g_t[:].bitcast(F32).rearrange("p (n u) -> p n u", u=2)
-                for pair in range(TILES // 2):
-                    h_turned = prod_t.tile([P, 2, 2 * P], F32, name="h_turned", tag="prod_t")
+            for pair in range(TILES // 2):
+                for s in range(PASSES):
+                    g_words = grouped_h[(nb, s)][:].bitcast(F32).rearrange("p (n u) -> p n u", u=2)
+                    h_turned = turned_pool.tile([P, 2, 2 * P], F32, name="h_turned", tag="turned")
                     for j in range(2):
                         nt = nb * TILES + 2 * pair + j
                         words = h_sb[:, nt, :].bitcast(F32).rearrange(
@@ -186,13 +196,14 @@ def tile_gatedgraphconvolution_pb_kernel(
                         out=g_words[:, n0 : n0 + 2 * P, :],
                         in_=h_turned[:].rearrange("p u n -> p n u"),
                     )
-                grouped[s] = g_t
+
+        def h_quantise(nb):
             nodes = slice(nb * HALF, (nb + 1) * HALF)
             for s in range(PASSES):
                 nc.vector.quantize_mx(
                     out=h_codes[:, s, nodes].bitcast(FP8X4),
                     scales=h_scales[:, s, nodes],
-                    in_=grouped[s][:],
+                    in_=grouped_h[(nb, s)][:],
                 )
 
         def mx_nodes_out(bank, cb, gate, nt):
@@ -244,12 +255,17 @@ def tile_gatedgraphconvolution_pb_kernel(
                     stop=(not adds_x) or t == TILES - 1,
                 )
 
+        r_prod = {}
+
         def r_product(i):
             b, q, cb, nb = split(i)
-            bank = prod_n.tile([P, HALF], F32, name="r_prod", tag="prod_n")
-            mx_nodes_out(bank, cb, R_GATE, nb * TILES + q)
+            r_prod[i] = prod_n.tile([P, HALF], F32, name="r_prod", tag="prod_n")
+            mx_nodes_out(r_prod[i], cb, R_GATE, nb * TILES + q)
+
+        def r_add(i):
+            b, q, cb, nb = split(i)
             ar[(b, q)] = ar_pool.tile([P, HALF], F32, name="ar", tag="ar")
-            nc.vector.tensor_add(out=ar[(b, q)][:], in0=bank[:], in1=x_tiles[i][:, R_GATE, :])
+            nc.vector.tensor_add(out=ar[(b, q)][:], in0=r_prod[i][:], in1=x_tiles[i][:, R_GATE, :])
 
         def r_turn(i):
             b, q, cb, nb = split(i)
@@ -262,7 +278,7 @@ def tile_gatedgraphconvolution_pb_kernel(
 
         def c_product(i):
             b, q, cb, nb = split(i)
-            c_prod[i] = prod_t.tile([P, HALF], F32, name="c_prod", tag="prod_t")
+            c_prod[i] = prod_c.tile([P, HALF], F32, name="c_prod", tag="prod_c")
             mx_cols_out(c_prod[i], cb, C_GATE, q, nb)
 
         def c_multiply(i):
@@ -301,23 +317,38 @@ def tile_gatedgraphconvolution_pb_kernel(
             z_tiles[i] = z_pool.tile([P, HALF], F32, name="z", tag="z")
             nc.scalar.activation(out=z_tiles[i][:], in_=bank[:], func=ACT.Sigmoid)
 
-        def mix(i):
+        mixes = {}
+
+        def mix_sub(i):
+            b, q, cb, nb = split(i)
+            mixes[i] = mix_pool.tile([P, HALF], F32, name="mix", tag="mix")
+            nc.vector.tensor_sub(
+                out=mixes[i][:],
+                in0=h_sb[:, nb * TILES + q, cb * HALF : (cb + 1) * HALF],
+                in1=cand[i][:],
+            )
+
+        def mix_mul(i):
+            nc.vector.tensor_mul(out=mixes[i][:], in0=mixes[i][:], in1=z_tiles[i][:])
+
+        def mix_add(i):
             b, q, cb, nb = split(i)
             nt = nb * TILES + q
-            cols = slice(cb * HALF, (cb + 1) * HALF)
-            m = mix_pool.tile([P, HALF], F32, name="mix", tag="mix")
-            nc.vector.tensor_sub(out=m[:], in0=h_sb[:, nt, cols], in1=cand[i][:])
-            nc.vector.tensor_mul(out=m[:], in0=m[:], in1=z_tiles[i][:])
-            nc.vector.tensor_add(out=m[:], in0=m[:], in1=cand[i][:])
-            nc.sync.dma_start(out=out_rows[nt * P : (nt + 1) * P, cols], in_=m[:])
+            nc.vector.tensor_add(out=mixes[i][:], in0=mixes[i][:], in1=cand[i][:])
+            nc.sync.dma_start(
+                out=out_rows[nt * P : (nt + 1) * P, cb * HALF : (cb + 1) * HALF], in_=mixes[i][:]
+            )
 
-        load_w(0, R_GATE)
+        ctx.enter_context(tc.manual_schedule(engines={mybir.EngineType.SP}))
         load_h(0)
-        for i in range(0, 4):
-            load_x(i)
+        load_w(0, R_GATE)
+        load_x(0)
+        load_x(1)
         load_w(0, Z_GATE)
-        load_w(0, C_GATE)
+        load_x(2)
+        load_x(3)
         load_h(1)
+        load_w(0, C_GATE)
         for i in range(4, 8):
             load_x(i)
         load_w(1, R_GATE)
@@ -325,28 +356,40 @@ def tile_gatedgraphconvolution_pb_kernel(
         load_w(1, C_GATE)
         for i in range(8, ITEMS):
             load_x(i)
+        h_transposes(0)
+        w_regroup(0, R_GATE)
+        h_quantise(0)
+        w_quantise(0, R_GATE)
 
-        prep_w(0, R_GATE)
-        prep_h(0)
-
-        for tick in range(ITEMS + MIX_LAG):
-            if is_item(tick - MIX_LAG):
-                mix(tick - MIX_LAG)
+        for tick in range(ITEMS + MIX_LAG + 1):
             if is_item(tick - C_TURN_LAG):
                 c_turn(tick - C_TURN_LAG)
             if is_item(tick - Z_TURN_LAG):
                 z_turn(tick - Z_TURN_LAG)
-            if is_item(tick - C_MX_LAG):
-                c_product(tick - C_MX_LAG)
-            if is_item(tick - C_MUL_LAG):
-                c_multiply(tick - C_MUL_LAG)
             if is_item(tick - R_TURN_LAG):
                 r_turn(tick - R_TURN_LAG)
-            if is_item(tick - Z_MX_LAG):
-                z_product(tick - Z_MX_LAG)
+            if tick in H_PREP:
+                h_transposes(H_PREP[tick])
             if is_item(tick):
                 r_product(tick)
-            if tick in H_PREP:
-                prep_h(H_PREP[tick])
+            if is_item(tick - C_MX_LAG):
+                c_product(tick - C_MX_LAG)
+            if is_item(tick - Z_MX_LAG):
+                z_product(tick - Z_MX_LAG)
+            m = tick - MIX_LAG
             if tick in W_PREP:
-                prep_w(W_PREP[tick][0], W_PREP[tick][1])
+                w_regroup(W_PREP[tick][0], W_PREP[tick][1])
+            if is_item(m):
+                mix_sub(m)
+            if is_item(tick - C_MUL_LAG):
+                c_multiply(tick - C_MUL_LAG)
+            if is_item(m):
+                mix_mul(m)
+            if is_item(tick - R_ADD_LAG):
+                r_add(tick - R_ADD_LAG)
+            if is_item(m):
+                mix_add(m)
+            if tick in H_PREP:
+                h_quantise(H_PREP[tick])
+            if tick in W_PREP:
+                w_quantise(W_PREP[tick][0], W_PREP[tick][1])

@@ -26,14 +26,17 @@ Z_GATE, R_GATE, C_GATE = 0, 1, 2
 
 FLOPS = 2 * NODES * C * 3 * C
 
+G = 2
+GN = G * P
+CT_PER_STEP = TILES // G
 R_ADD_LAG = 1
-R_TURN_LAG = 5
-C_MX_LAG = 5
-C_MUL_LAG = 6
-C_TURN_LAG = 10
+R_TURN_LAG = G + 1
+C_MX_LAG = G + 1
+C_MUL_LAG = G + 2
+C_TURN_LAG = 2 * G + 2
 Z_MX_LAG = 2
-Z_TURN_LAG = Z_MX_LAG + 5
-MIX_LAG = 11
+Z_TURN_LAG = Z_MX_LAG + G + 1
+MIX_LAG = 2 * G + 3
 S_PIECES = 4
 PSUM_R, PSUM_C, PSUM_Z, PSUM_TURNED = 2, 2, 1, 3
 ON_SCALAR = (
@@ -41,6 +44,9 @@ ON_SCALAR = (
 )
 W_PREP = {0: (0, Z_GATE), 2: (0, C_GATE), 5: (1, R_GATE), 7: (1, Z_GATE), 9: (1, C_GATE)}
 H_PREP = {1: 1}
+ON_GPSIMD = ()
+G_PIECES = 2
+ALTERNATE = False
 
 
 def tile_gatedgraphconvolution_pb_kernel(
@@ -56,13 +62,13 @@ def tile_gatedgraphconvolution_pb_kernel(
         w_raw_pool = ctx.enter_context(tc.tile_pool(name="w_raw", bufs=6))
         grouped_pool = ctx.enter_context(tc.tile_pool(name="grouped", bufs=5))
         x_pool = ctx.enter_context(tc.tile_pool(name="x", bufs=ITEMS))
-        ar_pool = ctx.enter_context(tc.tile_pool(name="ar", bufs=8))
+        ar_pool = ctx.enter_context(tc.tile_pool(name="ar", bufs=6))
         rt_pool = ctx.enter_context(tc.tile_pool(name="rt", bufs=3))
-        mt_pool = ctx.enter_context(tc.tile_pool(name="mt", bufs=8))
-        zb_pool = ctx.enter_context(tc.tile_pool(name="zb", bufs=8))
-        cand_pool = ctx.enter_context(tc.tile_pool(name="cand", bufs=3))
-        z_pool = ctx.enter_context(tc.tile_pool(name="z", bufs=7))
-        mix_pool = ctx.enter_context(tc.tile_pool(name="mix", bufs=4))
+        mt_pool = ctx.enter_context(tc.tile_pool(name="mt", bufs=6))
+        zb_pool = ctx.enter_context(tc.tile_pool(name="zb", bufs=7))
+        cand_pool = ctx.enter_context(tc.tile_pool(name="cand", bufs=5))
+        z_pool = ctx.enter_context(tc.tile_pool(name="z", bufs=8))
+        mix_pool = ctx.enter_context(tc.tile_pool(name="mix", bufs=5))
         prod_n = ctx.enter_context(tc.psum_pool(name="prod_n", bufs=PSUM_R))
         prod_t = ctx.enter_context(tc.psum_pool(name="prod_t", bufs=PSUM_Z))
         prod_c = ctx.enter_context(tc.psum_pool(name="prod_c", bufs=PSUM_C))
@@ -158,6 +164,14 @@ def tile_gatedgraphconvolution_pb_kernel(
                     for piece in range(S_PIECES):
                         part = slice(piece * step, (piece + 1) * step)
                         nc.scalar.copy(out=dst[:, part, :, :], in_=src[:, part, :, :])
+                elif (cb, gate, s) in ON_GPSIMD:
+                    step = HALF // 4 // G_PIECES
+                    for piece in range(G_PIECES):
+                        part = slice(piece * step, (piece + 1) * step)
+                        nc.gpsimd.tensor_scalar(
+                            out=dst[:, part, :, :], in0=src[:, part, :, :],
+                            scalar1=1.0, scalar2=0.0, op0=ALU.mult, op1=ALU.add,
+                        )
                 else:
                     nc.vector.tensor_copy(out=dst, in_=src)
                 grouped_w[(cb, gate, s)] = g_t
@@ -257,83 +271,131 @@ def tile_gatedgraphconvolution_pb_kernel(
 
         r_prod = {}
 
+        def place(i):
+            cb, nt = divmod(i, NODES // P)
+            return cb, nt, nt // G, nt % G
+
+        def step_place(u):
+            cb, rest = divmod(u, NODES // P)
+            return cb, rest // G, (rest % G) * CT_PER_STEP
+
         def r_product(i):
-            b, q, cb, nb = split(i)
+            cb, nt, g, j = place(i)
             r_prod[i] = prod_n.tile([P, HALF], F32, name="r_prod", tag="prod_n")
-            mx_nodes_out(r_prod[i], cb, R_GATE, nb * TILES + q)
+            mx_nodes_out(r_prod[i], cb, R_GATE, nt)
 
         def r_add(i):
-            b, q, cb, nb = split(i)
-            ar[(b, q)] = ar_pool.tile([P, HALF], F32, name="ar", tag="ar")
-            nc.vector.tensor_add(out=ar[(b, q)][:], in0=r_prod[i][:], in1=x_tiles[i][:, R_GATE, :])
+            ar[i] = ar_pool.tile([P, HALF], F32, name="ar", tag="ar")
+            nc.vector.tensor_add(out=ar[i][:], in0=r_prod[i][:], in1=x_tiles[i][:, R_GATE, :])
 
-        def r_turn(i):
-            b, q, cb, nb = split(i)
-            bank = turned_pool.tile([P, HALF], F32, name="r_bank", tag="turned")
-            turn(bank, ar, b, q, None)
-            rt[i] = rt_pool.tile([P, HALF], F32, name="rt", tag="rt")
-            nc.scalar.activation(
-                out=rt[i][:], in_=bank[:], func=ACT.Sigmoid, bias=bias_of(R_GATE, cb, q), scale=1.0
+        def r_turn(u):
+            cb, g, ct0 = step_place(u)
+            first = cb * (NODES // P) + g * G
+            bank = turned_pool.tile([P, CT_PER_STEP, GN], F32, name="r_bank", tag="turned")
+            rt[u] = rt_pool.tile([P, CT_PER_STEP, GN], F32, name="rt", tag="rt")
+            for c in range(CT_PER_STEP):
+                for t in range(G):
+                    nc.tensor.matmul(
+                        out=bank[:, c, t * P : (t + 1) * P],
+                        lhsT=ar[first + t][:, (ct0 + c) * P : (ct0 + c + 1) * P],
+                        rhs=ident_f32[:],
+                        is_transpose=True,
+                        start=True,
+                        stop=True,
+                    )
+            for c in range(CT_PER_STEP):
+                nc.scalar.activation(
+                    out=rt[u][:, c, :], in_=bank[:, c, :], func=ACT.Sigmoid,
+                    bias=bias_of(R_GATE, cb, ct0 + c), scale=1.0,
+                )
+
+        def cols_product(bank, u, gate):
+            cb, g, ct0 = step_place(u)
+            nodes = slice(g * GN, (g + 1) * GN)
+            for c in range(CT_PER_STEP):
+                cols = slice((ct0 + c) * P, (ct0 + c + 1) * P)
+                for s in range(PASSES):
+                    chunk = w_chunk(cb, gate, s)
+                    nc.tensor.matmul_mx(
+                        out=bank[:, c, :],
+                        lhsT=w_codes[:, chunk, cols].bitcast(FP8X4),
+                        lhsT_scale=w_scales[:, chunk, cols],
+                        rhs=h_codes[:, s, nodes].bitcast(FP8X4),
+                        rhs_scale=h_scales[:, s, nodes],
+                        start=(s == 0),
+                        stop=(s == PASSES - 1),
+                    )
+
+        def c_product(u):
+            c_prod[u] = prod_c.tile([P, CT_PER_STEP, GN], F32, name="c_prod", tag="prod_c")
+            cols_product(c_prod[u], u, C_GATE)
+
+        def c_multiply(u):
+            cb, g, ct0 = step_place(u)
+            mt[u] = mt_pool.tile([P, CT_PER_STEP, GN], F32, name="mt", tag="mt")
+            for c in range(CT_PER_STEP):
+                nc.vector.scalar_tensor_tensor(
+                    out=mt[u][:, c, :],
+                    in0=c_prod[u][:, c, :],
+                    scalar=bias_of(C_GATE, cb, ct0 + c),
+                    in1=rt[u][:, c, :],
+                    op0=ALU.add,
+                    op1=ALU.mult,
+                )
+
+        def z_product(u):
+            cb, g, ct0 = step_place(u)
+            bank = prod_t.tile([P, CT_PER_STEP, GN], F32, name="z_prod", tag="prod_t")
+            cols_product(bank, u, Z_GATE)
+            zb[u] = zb_pool.tile([P, CT_PER_STEP, GN], F32, name="zb", tag="zb")
+            for c in range(CT_PER_STEP):
+                nc.scalar.activation(
+                    out=zb[u][:, c, :], in_=bank[:, c, :], func=ACT.Identity,
+                    bias=bias_of(Z_GATE, cb, ct0 + c), scale=1.0,
+                )
+
+        def turn_back(bank, tiles, i, gate):
+            cb, nt, g, j = place(i)
+            first = cb * (NODES // P) + g * G
+            nc.tensor.matmul(
+                out=bank[:], lhsT=ident_bf16[:], rhs=x_tiles[i][:, gate, :], start=True, stop=False
             )
-
-        def c_product(i):
-            b, q, cb, nb = split(i)
-            c_prod[i] = prod_c.tile([P, HALF], F32, name="c_prod", tag="prod_c")
-            mx_cols_out(c_prod[i], cb, C_GATE, q, nb)
-
-        def c_multiply(i):
-            b, q, cb, nb = split(i)
-            mt[(b, q)] = mt_pool.tile([P, HALF], F32, name="mt", tag="mt")
-            nc.vector.scalar_tensor_tensor(
-                out=mt[(b, q)][:],
-                in0=c_prod[i][:],
-                scalar=bias_of(C_GATE, cb, q),
-                in1=rt[i][:],
-                op0=ALU.add,
-                op1=ALU.mult,
-            )
+            for ct in range(TILES):
+                nc.tensor.matmul(
+                    out=bank[:, ct * P : (ct + 1) * P],
+                    lhsT=tiles[first + ct // CT_PER_STEP][:, ct % CT_PER_STEP, j * P : (j + 1) * P],
+                    rhs=ident_f32[:],
+                    is_transpose=True,
+                    start=False,
+                    stop=ct == TILES - 1,
+                )
 
         def c_turn(i):
-            b, q, cb, nb = split(i)
             bank = turned_pool.tile([P, HALF], F32, name="c_bank", tag="turned")
-            turn(bank, mt, b, q, x_tiles[i][:, C_GATE, :])
+            turn_back(bank, mt, i, C_GATE)
             cand[i] = cand_pool.tile([P, HALF], F32, name="cand", tag="cand")
             nc.scalar.activation(out=cand[i][:], in_=bank[:], func=ACT.Tanh)
 
-        def z_product(i):
-            b, q, cb, nb = split(i)
-            bank = prod_t.tile([P, HALF], F32, name="z_prod", tag="prod_t")
-            mx_cols_out(bank, cb, Z_GATE, q, nb)
-            zb[(b, q)] = zb_pool.tile([P, HALF], F32, name="zb", tag="zb")
-            nc.scalar.activation(
-                out=zb[(b, q)][:], in_=bank[:], func=ACT.Identity,
-                bias=bias_of(Z_GATE, cb, q), scale=1.0,
-            )
-
         def z_turn(i):
-            b, q, cb, nb = split(i)
             bank = turned_pool.tile([P, HALF], F32, name="z_bank", tag="turned")
-            turn(bank, zb, b, q, x_tiles[i][:, Z_GATE, :])
+            turn_back(bank, zb, i, Z_GATE)
             z_tiles[i] = z_pool.tile([P, HALF], F32, name="z", tag="z")
             nc.scalar.activation(out=z_tiles[i][:], in_=bank[:], func=ACT.Sigmoid)
 
         mixes = {}
 
         def mix_sub(i):
-            b, q, cb, nb = split(i)
+            cb, nt, g, j = place(i)
             mixes[i] = mix_pool.tile([P, HALF], F32, name="mix", tag="mix")
             nc.vector.tensor_sub(
-                out=mixes[i][:],
-                in0=h_sb[:, nb * TILES + q, cb * HALF : (cb + 1) * HALF],
-                in1=cand[i][:],
+                out=mixes[i][:], in0=h_sb[:, nt, cb * HALF : (cb + 1) * HALF], in1=cand[i][:]
             )
 
         def mix_mul(i):
             nc.vector.tensor_mul(out=mixes[i][:], in0=mixes[i][:], in1=z_tiles[i][:])
 
         def mix_add(i):
-            b, q, cb, nb = split(i)
-            nt = nb * TILES + q
+            cb, nt, g, j = place(i)
             nc.vector.tensor_add(out=mixes[i][:], in0=mixes[i][:], in1=cand[i][:])
             nc.sync.dma_start(
                 out=out_rows[nt * P : (nt + 1) * P, cb * HALF : (cb + 1) * HALF], in_=mixes[i][:]
@@ -361,7 +423,7 @@ def tile_gatedgraphconvolution_pb_kernel(
         h_quantise(0)
         w_quantise(0, R_GATE)
 
-        for tick in range(ITEMS + MIX_LAG + 1):
+        def turn_run(tick):
             if is_item(tick - C_TURN_LAG):
                 c_turn(tick - C_TURN_LAG)
             if is_item(tick - Z_TURN_LAG):
@@ -370,12 +432,22 @@ def tile_gatedgraphconvolution_pb_kernel(
                 r_turn(tick - R_TURN_LAG)
             if tick in H_PREP:
                 h_transposes(H_PREP[tick])
+
+        def mx_run(tick):
             if is_item(tick):
                 r_product(tick)
             if is_item(tick - C_MX_LAG):
                 c_product(tick - C_MX_LAG)
             if is_item(tick - Z_MX_LAG):
                 z_product(tick - Z_MX_LAG)
+
+        for tick in range(ITEMS + MIX_LAG + 3):
+            if ALTERNATE and tick % 2 == 1:
+                mx_run(tick)
+                turn_run(tick)
+            else:
+                turn_run(tick)
+                mx_run(tick)
             m = tick - MIX_LAG
             if tick in W_PREP:
                 w_regroup(W_PREP[tick][0], W_PREP[tick][1])
@@ -383,12 +455,12 @@ def tile_gatedgraphconvolution_pb_kernel(
                 mix_sub(m)
             if is_item(tick - C_MUL_LAG):
                 c_multiply(tick - C_MUL_LAG)
-            if is_item(m):
-                mix_mul(m)
+            if is_item(m - 1):
+                mix_mul(m - 1)
             if is_item(tick - R_ADD_LAG):
                 r_add(tick - R_ADD_LAG)
-            if is_item(m):
-                mix_add(m)
+            if is_item(m - 2):
+                mix_add(m - 2)
             if tick in H_PREP:
                 h_quantise(H_PREP[tick])
             if tick in W_PREP:

@@ -43,10 +43,11 @@ ON_SCALAR = (
     (0, Z_GATE, 1), (0, C_GATE, 1), (1, R_GATE, 1), (1, Z_GATE, 1), (1, C_GATE, 1),
 )
 W_PREP = {0: (0, Z_GATE), 2: (0, C_GATE), 5: (1, R_GATE), 7: (1, Z_GATE), 9: (1, C_GATE)}
-H_PREP = {1: 1}
+H_PREP = {0: 1, 2: 2, 4: 3}
 ON_GPSIMD = ()
 G_PIECES = 2
 ALTERNATE = False
+NARROW_TAIL = 2
 
 
 def tile_gatedgraphconvolution_pb_kernel(
@@ -60,15 +61,16 @@ def tile_gatedgraphconvolution_pb_kernel(
         const = ctx.enter_context(tc.tile_pool(name="const", bufs=1))
         keep = ctx.enter_context(tc.tile_pool(name="keep", bufs=1))
         w_raw_pool = ctx.enter_context(tc.tile_pool(name="w_raw", bufs=6))
-        grouped_pool = ctx.enter_context(tc.tile_pool(name="grouped", bufs=5))
+        grouped_pool = ctx.enter_context(tc.tile_pool(name="grouped", bufs=4))
+        h_grouped_pool = ctx.enter_context(tc.tile_pool(name="h_grouped", bufs=4))
         x_pool = ctx.enter_context(tc.tile_pool(name="x", bufs=ITEMS))
         ar_pool = ctx.enter_context(tc.tile_pool(name="ar", bufs=6))
         rt_pool = ctx.enter_context(tc.tile_pool(name="rt", bufs=3))
         mt_pool = ctx.enter_context(tc.tile_pool(name="mt", bufs=6))
         zb_pool = ctx.enter_context(tc.tile_pool(name="zb", bufs=7))
-        cand_pool = ctx.enter_context(tc.tile_pool(name="cand", bufs=5))
-        z_pool = ctx.enter_context(tc.tile_pool(name="z", bufs=8))
-        mix_pool = ctx.enter_context(tc.tile_pool(name="mix", bufs=5))
+        cand_pool = ctx.enter_context(tc.tile_pool(name="cand", bufs=3))
+        z_pool = ctx.enter_context(tc.tile_pool(name="z", bufs=4))
+        mix_pool = ctx.enter_context(tc.tile_pool(name="mix", bufs=3))
         prod_n = ctx.enter_context(tc.psum_pool(name="prod_n", bufs=PSUM_R))
         prod_t = ctx.enter_context(tc.psum_pool(name="prod_t", bufs=PSUM_Z))
         prod_c = ctx.enter_context(tc.psum_pool(name="prod_c", bufs=PSUM_C))
@@ -122,21 +124,20 @@ def tile_gatedgraphconvolution_pb_kernel(
         def is_item(i):
             return 0 <= i < ITEMS
 
-        def load_w(cb, gate):
+        def load_w(cb, gate, passes=(0, 1)):
             col0 = gate * C + cb * HALF
-            for s in range(PASSES):
+            for s in passes:
                 raw = w_raw_pool.tile([P, PACK, HALF], BF16, name="w_raw", tag="w_raw")
                 rows = recurrent_kernel[s * K_PASS : (s + 1) * K_PASS, col0 : col0 + HALF]
                 nc.sync.dma_start(out=raw[:], in_=rows.rearrange("(p t) c -> p t c", t=PACK))
                 w_raw[(cb, gate, s)] = raw
 
-        def load_h(nb):
-            for half in range(2):
-                nt0 = nb * TILES + 2 * half
-                rows = h_rows[nt0 * P : (nt0 + 2) * P, :]
-                nc.sync.dma_start(
-                    out=h_sb[:, nt0 : nt0 + 2, :], in_=rows.rearrange("(t p) c -> p t c", p=P)
-                )
+        def load_h(hg):
+            nt0 = 2 * hg
+            rows = h_rows[nt0 * P : (nt0 + 2) * P, :]
+            nc.sync.dma_start(
+                out=h_sb[:, nt0 : nt0 + 2, :], in_=rows.rearrange("(t p) c -> p t c", p=P)
+            )
 
         def load_x(i):
             b, q, cb, nb = split(i)
@@ -185,39 +186,32 @@ def tile_gatedgraphconvolution_pb_kernel(
                     in_=grouped_w[(cb, gate, s)][:],
                 )
 
-        def h_transposes(nb):
+        def h_transposes(hg):
             for s in range(PASSES):
-                grouped_h[(nb, s)] = grouped_pool.tile(
-                    [P, HALF * PACK], BF16, name="grouped", tag="grouped", align_bytes=64
+                grouped_h[(hg, s)] = h_grouped_pool.tile(
+                    [P, 2 * P * PACK], BF16, name="h_grouped", tag="h_grouped", align_bytes=64
                 )
-            for pair in range(TILES // 2):
-                for s in range(PASSES):
-                    g_words = grouped_h[(nb, s)][:].bitcast(F32).rearrange("p (n u) -> p n u", u=2)
-                    h_turned = turned_pool.tile([P, 2, 2 * P], F32, name="h_turned", tag="turned")
-                    for j in range(2):
-                        nt = nb * TILES + 2 * pair + j
-                        words = h_sb[:, nt, :].bitcast(F32).rearrange(
-                            "p (s w u) -> p s u w", s=PASSES, u=2
-                        )
-                        for u in range(2):
-                            nc.tensor.transpose(
-                                out=h_turned[:, u, j * P : (j + 1) * P],
-                                in_=words[:, s, u, :],
-                                identity=ident_f32[:],
-                            )
-                    n0 = pair * 2 * P
-                    nc.scalar.copy(
-                        out=g_words[:, n0 : n0 + 2 * P, :],
-                        in_=h_turned[:].rearrange("p u n -> p n u"),
+                g_words = grouped_h[(hg, s)][:].bitcast(F32).rearrange("p (n u) -> p n u", u=2)
+                h_turned = turned_pool.tile([P, 2, 2 * P], F32, name="h_turned", tag="turned")
+                for j in range(2):
+                    words = h_sb[:, 2 * hg + j, :].bitcast(F32).rearrange(
+                        "p (s w u) -> p s u w", s=PASSES, u=2
                     )
+                    for u in range(2):
+                        nc.tensor.transpose(
+                            out=h_turned[:, u, j * P : (j + 1) * P],
+                            in_=words[:, s, u, :],
+                            identity=ident_f32[:],
+                        )
+                nc.scalar.copy(out=g_words, in_=h_turned[:].rearrange("p u n -> p n u"))
 
-        def h_quantise(nb):
-            nodes = slice(nb * HALF, (nb + 1) * HALF)
+        def h_quantise(hg):
+            nodes = slice(hg * 2 * P, (hg + 1) * 2 * P)
             for s in range(PASSES):
                 nc.vector.quantize_mx(
                     out=h_codes[:, s, nodes].bitcast(FP8X4),
                     scales=h_scales[:, s, nodes],
-                    in_=grouped_h[(nb, s)][:],
+                    in_=grouped_h[(hg, s)][:],
                 )
 
         def mx_nodes_out(bank, cb, gate, nt):
@@ -373,46 +367,72 @@ def tile_gatedgraphconvolution_pb_kernel(
         def c_turn(i):
             bank = turned_pool.tile([P, HALF], F32, name="c_bank", tag="turned")
             turn_back(bank, mt, i, C_GATE)
-            cand[i] = cand_pool.tile([P, HALF], F32, name="cand", tag="cand")
-            nc.scalar.activation(out=cand[i][:], in_=bank[:], func=ACT.Tanh)
+            cb, nt, g, j = place(i)
+            if j == 0:
+                cand[i // G] = cand_pool.tile([P, G, HALF], F32, name="cand", tag="cand")
+            nc.scalar.activation(out=cand[i // G][:, j, :], in_=bank[:], func=ACT.Tanh)
 
         def z_turn(i):
             bank = turned_pool.tile([P, HALF], F32, name="z_bank", tag="turned")
             turn_back(bank, zb, i, Z_GATE)
-            z_tiles[i] = z_pool.tile([P, HALF], F32, name="z", tag="z")
-            nc.scalar.activation(out=z_tiles[i][:], in_=bank[:], func=ACT.Sigmoid)
+            cb, nt, g, j = place(i)
+            if j == 0:
+                z_tiles[i // G] = z_pool.tile([P, G, HALF], F32, name="z", tag="z")
+            nc.scalar.activation(out=z_tiles[i // G][:, j, :], in_=bank[:], func=ACT.Sigmoid)
 
         mixes = {}
 
-        def mix_sub(i):
-            cb, nt, g, j = place(i)
-            mixes[i] = mix_pool.tile([P, HALF], F32, name="mix", tag="mix")
-            nc.vector.tensor_sub(
-                out=mixes[i][:], in0=h_sb[:, nt, cb * HALF : (cb + 1) * HALF], in1=cand[i][:]
+        def span(first, count):
+            cb, nt, g, j = place(first)
+            w = first // G
+            cols = slice(cb * HALF, (cb + 1) * HALF)
+            return (
+                mixes[w][:, j : j + count, :],
+                h_sb[:, nt : nt + count, cols],
+                cand[w][:, j : j + count, :],
+                z_tiles[w][:, j : j + count, :],
+                out_rows[nt * P : (nt + count) * P, cols].rearrange("(t p) c -> p t c", p=P),
             )
 
-        def mix_mul(i):
-            nc.vector.tensor_mul(out=mixes[i][:], in0=mixes[i][:], in1=z_tiles[i][:])
+        def mix_sub(first, count):
+            if first % G == 0:
+                mixes[first // G] = mix_pool.tile([P, G, HALF], F32, name="mix", tag="mix")
+            m_ap, h_ap, c_ap, z_ap, o_ap = span(first, count)
+            nc.vector.tensor_sub(out=m_ap, in0=h_ap, in1=c_ap)
 
-        def mix_add(i):
-            cb, nt, g, j = place(i)
-            nc.vector.tensor_add(out=mixes[i][:], in0=mixes[i][:], in1=cand[i][:])
-            nc.sync.dma_start(
-                out=out_rows[nt * P : (nt + 1) * P, cb * HALF : (cb + 1) * HALF], in_=mixes[i][:]
-            )
+        def mix_mul(first, count):
+            m_ap, h_ap, c_ap, z_ap, o_ap = span(first, count)
+            nc.vector.tensor_mul(out=m_ap, in0=m_ap, in1=z_ap)
+
+        def mix_add(first, count):
+            m_ap, h_ap, c_ap, z_ap, o_ap = span(first, count)
+            nc.vector.tensor_add(out=m_ap, in0=m_ap, in1=c_ap)
+            nc.sync.dma_start(out=o_ap, in_=m_ap)
+
+        def mix_work(m):
+            if not is_item(m):
+                return None
+            if m >= ITEMS - NARROW_TAIL:
+                return (m, 1)
+            return (m - G + 1, G) if m % G == G - 1 else None
 
         ctx.enter_context(tc.manual_schedule(engines={mybir.EngineType.SP}))
+        load_w(0, R_GATE, (0,))
         load_h(0)
-        load_w(0, R_GATE)
+        load_w(0, R_GATE, (1,))
         load_x(0)
         load_x(1)
+        load_h(1)
         load_w(0, Z_GATE)
         load_x(2)
         load_x(3)
-        load_h(1)
         load_w(0, C_GATE)
-        for i in range(4, 8):
-            load_x(i)
+        load_h(2)
+        load_x(4)
+        load_x(5)
+        load_h(3)
+        load_x(6)
+        load_x(7)
         load_w(1, R_GATE)
         load_w(1, Z_GATE)
         load_w(1, C_GATE)
@@ -451,16 +471,16 @@ def tile_gatedgraphconvolution_pb_kernel(
             m = tick - MIX_LAG
             if tick in W_PREP:
                 w_regroup(W_PREP[tick][0], W_PREP[tick][1])
-            if is_item(m):
-                mix_sub(m)
+            if mix_work(m) is not None:
+                mix_sub(mix_work(m)[0], mix_work(m)[1])
             if is_item(tick - C_MUL_LAG):
                 c_multiply(tick - C_MUL_LAG)
-            if is_item(m - 1):
-                mix_mul(m - 1)
+            if mix_work(m - 1) is not None:
+                mix_mul(mix_work(m - 1)[0], mix_work(m - 1)[1])
             if is_item(tick - R_ADD_LAG):
                 r_add(tick - R_ADD_LAG)
-            if is_item(m - 2):
-                mix_add(m - 2)
+            if mix_work(m - 2) is not None:
+                mix_add(mix_work(m - 2)[0], mix_work(m - 2)[1])
             if tick in H_PREP:
                 h_quantise(H_PREP[tick])
             if tick in W_PREP:

@@ -19,35 +19,17 @@ C = 1024
 PASSES = C // K_PASS
 HALF = 512
 TILES = HALF // P
-BLOCKS = 4
-ITEMS = BLOCKS * TILES
 
 Z_GATE, R_GATE, C_GATE = 0, 1, 2
 
 FLOPS = 2 * NODES * C * 3 * C
 
-G = 2
-GN = G * P
-CT_PER_STEP = TILES // G
-R_ADD_LAG = 1
-R_TURN_LAG = G + 1
-C_MX_LAG = G + 1
-C_MUL_LAG = G + 2
-C_TURN_LAG = 2 * G + 2
-Z_MX_LAG = 2
-Z_TURN_LAG = Z_MX_LAG + G + 1
-MIX_LAG = 2 * G + 3
 S_PIECES = 4
-PSUM_R, PSUM_C, PSUM_Z, PSUM_TURNED = 2, 2, 1, 3
 ON_SCALAR = (
     (0, Z_GATE, 1), (0, C_GATE, 1), (1, R_GATE, 1), (1, Z_GATE, 1), (1, C_GATE, 1),
 )
-W_PREP = {0: (0, Z_GATE), 2: (0, C_GATE), 5: (1, R_GATE), 7: (1, Z_GATE), 9: (1, C_GATE)}
-H_PREP = {0: 1, 2: 2, 4: 3}
-ON_GPSIMD = ()
-G_PIECES = 2
-ALTERNATE = False
-NARROW_TAIL = 2
+IDS_TOGETHER = False
+PIN = ()
 
 
 def tile_gatedgraphconvolution_pb_kernel(
@@ -61,20 +43,20 @@ def tile_gatedgraphconvolution_pb_kernel(
         const = ctx.enter_context(tc.tile_pool(name="const", bufs=1))
         keep = ctx.enter_context(tc.tile_pool(name="keep", bufs=1))
         w_raw_pool = ctx.enter_context(tc.tile_pool(name="w_raw", bufs=6))
-        grouped_pool = ctx.enter_context(tc.tile_pool(name="grouped", bufs=4))
+        grouped_pool = ctx.enter_context(tc.tile_pool(name="grouped", bufs=3))
         h_grouped_pool = ctx.enter_context(tc.tile_pool(name="h_grouped", bufs=4))
-        x_pool = ctx.enter_context(tc.tile_pool(name="x", bufs=ITEMS))
-        ar_pool = ctx.enter_context(tc.tile_pool(name="ar", bufs=6))
-        rt_pool = ctx.enter_context(tc.tile_pool(name="rt", bufs=3))
+        x_pool = ctx.enter_context(tc.tile_pool(name="x", bufs=8))
+        ar_pool = ctx.enter_context(tc.tile_pool(name="ar", bufs=8))
+        rt_pool = ctx.enter_context(tc.tile_pool(name="rt", bufs=8))
         mt_pool = ctx.enter_context(tc.tile_pool(name="mt", bufs=6))
-        zb_pool = ctx.enter_context(tc.tile_pool(name="zb", bufs=7))
-        cand_pool = ctx.enter_context(tc.tile_pool(name="cand", bufs=3))
+        zb_pool = ctx.enter_context(tc.tile_pool(name="zb", bufs=6))
+        cand_pool = ctx.enter_context(tc.tile_pool(name="cand", bufs=4))
         z_pool = ctx.enter_context(tc.tile_pool(name="z", bufs=4))
         mix_pool = ctx.enter_context(tc.tile_pool(name="mix", bufs=3))
-        prod_n = ctx.enter_context(tc.psum_pool(name="prod_n", bufs=PSUM_R))
-        prod_t = ctx.enter_context(tc.psum_pool(name="prod_t", bufs=PSUM_Z))
-        prod_c = ctx.enter_context(tc.psum_pool(name="prod_c", bufs=PSUM_C))
-        turned_pool = ctx.enter_context(tc.psum_pool(name="turned", bufs=PSUM_TURNED))
+        psum = ctx.enter_context(tc.psum_pool(name="psum", bufs=8))
+
+        def bank(shape, dtype=F32):
+            return psum.tile(shape, dtype, name="bank", tag="bank")
 
         ident_f32 = const.tile([P, P], F32, name="ident_f32")
         make_identity(nc, ident_f32[:])
@@ -91,7 +73,7 @@ def tile_gatedgraphconvolution_pb_kernel(
         nc.sync.dma_start(
             out=bias_rows[0:bias_tiles, :], in_=bias_h.rearrange("(j p) -> j p", p=P)
         )
-        bias_turned = turned_pool.tile([P, P], BF16, name="bias_turned", tag="turned")
+        bias_turned = bank([P, P], BF16)
         nc.tensor.transpose(out=bias_turned[:], in_=bias_rows[:], identity=ident_bf16[:])
         bias_col = const.tile([P, bias_tiles], F32, name="bias_col")
         nc.vector.tensor_copy(out=bias_col[:], in_=bias_turned[:, 0:bias_tiles])
@@ -108,21 +90,8 @@ def tile_gatedgraphconvolution_pb_kernel(
 
         w_raw = {}
         x_tiles = {}
-        ar = {}
-        rt = {}
-        c_prod = {}
-        mt = {}
-        zb = {}
-        cand = {}
-        z_tiles = {}
-
-        def split(i):
-            b, q = divmod(i, TILES)
-            cb, nb = divmod(b, 2)
-            return b, q, cb, nb
-
-        def is_item(i):
-            return 0 <= i < ITEMS
+        grouped_w = {}
+        grouped_h = {}
 
         def load_w(cb, gate, passes=(0, 1)):
             col0 = gate * C + cb * HALF
@@ -139,19 +108,12 @@ def tile_gatedgraphconvolution_pb_kernel(
                 out=h_sb[:, nt0 : nt0 + 2, :], in_=rows.rearrange("(t p) c -> p t c", p=P)
             )
 
-        def load_x(i):
-            b, q, cb, nb = split(i)
-            nt = nb * TILES + q
-            x_t = x_pool.tile([P, 3, HALF], BF16, name="x_t", tag="x_t")
-            rows = x_proj[nt * P : (nt + 1) * P, :]
-            nc.sync.dma_start(
-                out=x_t[:],
-                in_=rows.rearrange("p (g c) -> p g c", g=3)[:, :, cb * HALF : (cb + 1) * HALF],
-            )
-            x_tiles[i] = x_t
-
-        grouped_w = {}
-        grouped_h = {}
+        def load_x(cb, gate, nb):
+            x_t = x_pool.tile([P, TILES, HALF], BF16, name="x_t", tag="x_t")
+            col0 = gate * C + cb * HALF
+            rows = x_proj[nb * HALF : (nb + 1) * HALF, col0 : col0 + HALF]
+            nc.sync.dma_start(out=x_t[:], in_=rows.rearrange("(j p) c -> p j c", p=P))
+            x_tiles[(cb, gate, nb)] = x_t
 
         def w_regroup(cb, gate):
             for s in range(PASSES):
@@ -165,14 +127,6 @@ def tile_gatedgraphconvolution_pb_kernel(
                     for piece in range(S_PIECES):
                         part = slice(piece * step, (piece + 1) * step)
                         nc.scalar.copy(out=dst[:, part, :, :], in_=src[:, part, :, :])
-                elif (cb, gate, s) in ON_GPSIMD:
-                    step = HALF // 4 // G_PIECES
-                    for piece in range(G_PIECES):
-                        part = slice(piece * step, (piece + 1) * step)
-                        nc.gpsimd.tensor_scalar(
-                            out=dst[:, part, :, :], in0=src[:, part, :, :],
-                            scalar1=1.0, scalar2=0.0, op0=ALU.mult, op1=ALU.add,
-                        )
                 else:
                     nc.vector.tensor_copy(out=dst, in_=src)
                 grouped_w[(cb, gate, s)] = g_t
@@ -192,7 +146,7 @@ def tile_gatedgraphconvolution_pb_kernel(
                     [P, 2 * P * PACK], BF16, name="h_grouped", tag="h_grouped", align_bytes=64
                 )
                 g_words = grouped_h[(hg, s)][:].bitcast(F32).rearrange("p (n u) -> p n u", u=2)
-                h_turned = turned_pool.tile([P, 2, 2 * P], F32, name="h_turned", tag="turned")
+                h_turned = bank([P, 2, 2 * P])
                 for j in range(2):
                     words = h_sb[:, 2 * hg + j, :].bitcast(F32).rearrange(
                         "p (s w u) -> p s u w", s=PASSES, u=2
@@ -214,12 +168,12 @@ def tile_gatedgraphconvolution_pb_kernel(
                     in_=grouped_h[(hg, s)][:],
                 )
 
-        def mx_nodes_out(bank, cb, gate, nt):
+        def mx_nodes_out(bk, cb, gate, nt):
             nodes = slice(nt * P, (nt + 1) * P)
             for s in range(PASSES):
                 chunk = w_chunk(cb, gate, s)
                 nc.tensor.matmul_mx(
-                    out=bank[:],
+                    out=bk[:],
                     lhsT=h_codes[:, s, nodes].bitcast(FP8X4),
                     lhsT_scale=h_scales[:, s, nodes],
                     rhs=w_codes[:, chunk, :].bitcast(FP8X4),
@@ -228,13 +182,13 @@ def tile_gatedgraphconvolution_pb_kernel(
                     stop=(s == PASSES - 1),
                 )
 
-        def mx_cols_out(bank, cb, gate, ct, nb):
+        def mx_cols_out(bk, cb, gate, ct, nb):
             nodes = slice(nb * HALF, (nb + 1) * HALF)
             cols = slice(ct * P, (ct + 1) * P)
             for s in range(PASSES):
                 chunk = w_chunk(cb, gate, s)
                 nc.tensor.matmul_mx(
-                    out=bank[:],
+                    out=bk[:],
                     lhsT=w_codes[:, chunk, cols].bitcast(FP8X4),
                     lhsT_scale=w_scales[:, chunk, cols],
                     rhs=h_codes[:, s, nodes].bitcast(FP8X4),
@@ -247,241 +201,227 @@ def tile_gatedgraphconvolution_pb_kernel(
             j = gate * (C // P) + cb * TILES + ct
             return bias_col[:, j : j + 1]
 
-        def turn(bank, tiles, b, q, x_block):
-            adds_x = x_block is not None
-            if adds_x:
+        ar = {}
+        rt = {}
+        mt = {}
+        zb = {}
+        cand = {}
+        z_tiles = {}
+        mixes = {}
+
+        def r_product(cb, nt):
+            nb, j = divmod(nt, TILES)
+            bk = bank([P, HALF])
+            mx_nodes_out(bk, cb, R_GATE, nt)
+            ar[(cb, nt)] = ar_pool.tile([P, HALF], F32, name="ar", tag="ar")
+            nc.vector.tensor_add(out=ar[(cb, nt)][:], in0=bk[:], in1=x_tiles[(cb, R_GATE, nb)][:, j, :])
+
+        def r_turn(cb, nb, ct):
+            bk = bank([P, HALF])
+            for j in range(TILES):
                 nc.tensor.matmul(
-                    out=bank[:], lhsT=ident_bf16[:], rhs=x_block, start=True, stop=False
-                )
-            for t in range(TILES):
-                nc.tensor.matmul(
-                    out=bank[:, t * P : (t + 1) * P],
-                    lhsT=tiles[(b, t)][:, q * P : (q + 1) * P],
+                    out=bk[:, j * P : (j + 1) * P],
+                    lhsT=ar[(cb, nb * TILES + j)][:, ct * P : (ct + 1) * P],
                     rhs=ident_f32[:],
                     is_transpose=True,
-                    start=not adds_x,
-                    stop=(not adds_x) or t == TILES - 1,
+                    start=True,
+                    stop=True,
                 )
-
-        r_prod = {}
-
-        def place(i):
-            cb, nt = divmod(i, NODES // P)
-            return cb, nt, nt // G, nt % G
-
-        def step_place(u):
-            cb, rest = divmod(u, NODES // P)
-            return cb, rest // G, (rest % G) * CT_PER_STEP
-
-        def r_product(i):
-            cb, nt, g, j = place(i)
-            r_prod[i] = prod_n.tile([P, HALF], F32, name="r_prod", tag="prod_n")
-            mx_nodes_out(r_prod[i], cb, R_GATE, nt)
-
-        def r_add(i):
-            ar[i] = ar_pool.tile([P, HALF], F32, name="ar", tag="ar")
-            nc.vector.tensor_add(out=ar[i][:], in0=r_prod[i][:], in1=x_tiles[i][:, R_GATE, :])
-
-        def r_turn(u):
-            cb, g, ct0 = step_place(u)
-            first = cb * (NODES // P) + g * G
-            bank = turned_pool.tile([P, CT_PER_STEP, GN], F32, name="r_bank", tag="turned")
-            rt[u] = rt_pool.tile([P, CT_PER_STEP, GN], F32, name="rt", tag="rt")
-            for c in range(CT_PER_STEP):
-                for t in range(G):
-                    nc.tensor.matmul(
-                        out=bank[:, c, t * P : (t + 1) * P],
-                        lhsT=ar[first + t][:, (ct0 + c) * P : (ct0 + c + 1) * P],
-                        rhs=ident_f32[:],
-                        is_transpose=True,
-                        start=True,
-                        stop=True,
-                    )
-            for c in range(CT_PER_STEP):
-                nc.scalar.activation(
-                    out=rt[u][:, c, :], in_=bank[:, c, :], func=ACT.Sigmoid,
-                    bias=bias_of(R_GATE, cb, ct0 + c), scale=1.0,
-                )
-
-        def cols_product(bank, u, gate):
-            cb, g, ct0 = step_place(u)
-            nodes = slice(g * GN, (g + 1) * GN)
-            for c in range(CT_PER_STEP):
-                cols = slice((ct0 + c) * P, (ct0 + c + 1) * P)
-                for s in range(PASSES):
-                    chunk = w_chunk(cb, gate, s)
-                    nc.tensor.matmul_mx(
-                        out=bank[:, c, :],
-                        lhsT=w_codes[:, chunk, cols].bitcast(FP8X4),
-                        lhsT_scale=w_scales[:, chunk, cols],
-                        rhs=h_codes[:, s, nodes].bitcast(FP8X4),
-                        rhs_scale=h_scales[:, s, nodes],
-                        start=(s == 0),
-                        stop=(s == PASSES - 1),
-                    )
-
-        def c_product(u):
-            c_prod[u] = prod_c.tile([P, CT_PER_STEP, GN], F32, name="c_prod", tag="prod_c")
-            cols_product(c_prod[u], u, C_GATE)
-
-        def c_multiply(u):
-            cb, g, ct0 = step_place(u)
-            mt[u] = mt_pool.tile([P, CT_PER_STEP, GN], F32, name="mt", tag="mt")
-            for c in range(CT_PER_STEP):
-                nc.vector.scalar_tensor_tensor(
-                    out=mt[u][:, c, :],
-                    in0=c_prod[u][:, c, :],
-                    scalar=bias_of(C_GATE, cb, ct0 + c),
-                    in1=rt[u][:, c, :],
-                    op0=ALU.add,
-                    op1=ALU.mult,
-                )
-
-        def z_product(u):
-            cb, g, ct0 = step_place(u)
-            bank = prod_t.tile([P, CT_PER_STEP, GN], F32, name="z_prod", tag="prod_t")
-            cols_product(bank, u, Z_GATE)
-            zb[u] = zb_pool.tile([P, CT_PER_STEP, GN], F32, name="zb", tag="zb")
-            for c in range(CT_PER_STEP):
-                nc.scalar.activation(
-                    out=zb[u][:, c, :], in_=bank[:, c, :], func=ACT.Identity,
-                    bias=bias_of(Z_GATE, cb, ct0 + c), scale=1.0,
-                )
-
-        def turn_back(bank, tiles, i, gate):
-            cb, nt, g, j = place(i)
-            first = cb * (NODES // P) + g * G
-            nc.tensor.matmul(
-                out=bank[:], lhsT=ident_bf16[:], rhs=x_tiles[i][:, gate, :], start=True, stop=False
+            rt[(cb, nb, ct)] = rt_pool.tile([P, HALF], F32, name="rt", tag="rt")
+            nc.scalar.activation(
+                out=rt[(cb, nb, ct)][:], in_=bk[:], func=ACT.Sigmoid,
+                bias=bias_of(R_GATE, cb, ct), scale=1.0,
             )
+
+        def z_product(cb, nb, ct):
+            bk = bank([P, HALF])
+            mx_cols_out(bk, cb, Z_GATE, ct, nb)
+            zb[(cb, nb, ct)] = zb_pool.tile([P, HALF], F32, name="zb", tag="zb")
+            nc.scalar.activation(
+                out=zb[(cb, nb, ct)][:], in_=bk[:], func=ACT.Identity,
+                bias=bias_of(Z_GATE, cb, ct), scale=1.0,
+            )
+
+        def c_product(cb, nb, ct):
+            bk = bank([P, HALF])
+            mx_cols_out(bk, cb, C_GATE, ct, nb)
+            mt[(cb, nb, ct)] = mt_pool.tile([P, HALF], F32, name="mt", tag="mt")
+            nc.vector.scalar_tensor_tensor(
+                out=mt[(cb, nb, ct)][:],
+                in0=bk[:],
+                scalar=bias_of(C_GATE, cb, ct),
+                in1=rt[(cb, nb, ct)][:],
+                op0=ALU.add,
+                op1=ALU.mult,
+            )
+
+        def back_open(cb, gate, nb, j):
+            bk = bank([P, HALF])
+            nc.tensor.matmul(
+                out=bk[:], lhsT=ident_bf16[:], rhs=x_tiles[(cb, gate, nb)][:, j, :],
+                start=True, stop=False,
+            )
+            return bk
+
+        def back_turn(bk, tiles, cb, nb, j):
             for ct in range(TILES):
                 nc.tensor.matmul(
-                    out=bank[:, ct * P : (ct + 1) * P],
-                    lhsT=tiles[first + ct // CT_PER_STEP][:, ct % CT_PER_STEP, j * P : (j + 1) * P],
+                    out=bk[:, ct * P : (ct + 1) * P],
+                    lhsT=tiles[(cb, nb, ct)][:, j * P : (j + 1) * P],
                     rhs=ident_f32[:],
                     is_transpose=True,
                     start=False,
                     stop=ct == TILES - 1,
                 )
 
-        def c_turn(i):
-            bank = turned_pool.tile([P, HALF], F32, name="c_bank", tag="turned")
-            turn_back(bank, mt, i, C_GATE)
-            cb, nt, g, j = place(i)
-            if j == 0:
-                cand[i // G] = cand_pool.tile([P, G, HALF], F32, name="cand", tag="cand")
-            nc.scalar.activation(out=cand[i // G][:, j, :], in_=bank[:], func=ACT.Tanh)
+        def finish(bk, store, pool, name, func, cb, nb, j):
+            if j % 2 == 0:
+                store[(cb, nb, j // 2)] = pool.tile([P, 2, HALF], F32, name=name, tag=name)
+            nc.scalar.activation(out=store[(cb, nb, j // 2)][:, j % 2, :], in_=bk[:], func=func)
 
-        def z_turn(i):
-            bank = turned_pool.tile([P, HALF], F32, name="z_bank", tag="turned")
-            turn_back(bank, zb, i, Z_GATE)
-            cb, nt, g, j = place(i)
-            if j == 0:
-                z_tiles[i // G] = z_pool.tile([P, G, HALF], F32, name="z", tag="z")
-            nc.scalar.activation(out=z_tiles[i // G][:, j, :], in_=bank[:], func=ACT.Sigmoid)
+        def turn_backs(cb, nb):
+            if IDS_TOGETHER:
+                zbk = [back_open(cb, Z_GATE, nb, j) for j in range(TILES)]
+                cbk = [back_open(cb, C_GATE, nb, j) for j in range(TILES)]
+            else:
+                zbk = [back_open(cb, Z_GATE, nb, j) for j in range(TILES)]
+            for j in range(TILES):
+                back_turn(zbk[j], zb, cb, nb, j)
+                finish(zbk[j], z_tiles, z_pool, "z", ACT.Sigmoid, cb, nb, j)
+            if not IDS_TOGETHER:
+                cbk = [back_open(cb, C_GATE, nb, j) for j in range(TILES)]
+            for j in range(TILES):
+                back_turn(cbk[j], mt, cb, nb, j)
+                finish(cbk[j], cand, cand_pool, "cand", ACT.Tanh, cb, nb, j)
 
-        mixes = {}
-
-        def span(first, count):
-            cb, nt, g, j = place(first)
-            w = first // G
+        def span(b, j, count):
+            cb, nb = b
+            w = (cb, nb, j // 2)
+            nt = nb * TILES + j
             cols = slice(cb * HALF, (cb + 1) * HALF)
+            k = j % 2
             return (
-                mixes[w][:, j : j + count, :],
+                mixes[w][:, k : k + count, :],
                 h_sb[:, nt : nt + count, cols],
-                cand[w][:, j : j + count, :],
-                z_tiles[w][:, j : j + count, :],
+                cand[w][:, k : k + count, :],
+                z_tiles[w][:, k : k + count, :],
                 out_rows[nt * P : (nt + count) * P, cols].rearrange("(t p) c -> p t c", p=P),
             )
 
-        def mix_sub(first, count):
-            if first % G == 0:
-                mixes[first // G] = mix_pool.tile([P, G, HALF], F32, name="mix", tag="mix")
-            m_ap, h_ap, c_ap, z_ap, o_ap = span(first, count)
+        def mix_sub(b, j, count):
+            if j % 2 == 0:
+                mixes[(b[0], b[1], j // 2)] = mix_pool.tile([P, 2, HALF], F32, name="mix", tag="mix")
+            m_ap, h_ap, c_ap, z_ap, o_ap = span(b, j, count)
             nc.vector.tensor_sub(out=m_ap, in0=h_ap, in1=c_ap)
 
-        def mix_mul(first, count):
-            m_ap, h_ap, c_ap, z_ap, o_ap = span(first, count)
+        def mix_mul(b, j, count):
+            m_ap, h_ap, c_ap, z_ap, o_ap = span(b, j, count)
             nc.vector.tensor_mul(out=m_ap, in0=m_ap, in1=z_ap)
 
-        def mix_add(first, count):
-            m_ap, h_ap, c_ap, z_ap, o_ap = span(first, count)
+        def mix_add(b, j, count):
+            m_ap, h_ap, c_ap, z_ap, o_ap = span(b, j, count)
             nc.vector.tensor_add(out=m_ap, in0=m_ap, in1=c_ap)
             nc.sync.dma_start(out=o_ap, in_=m_ap)
 
-        def mix_work(m):
-            if not is_item(m):
-                return None
-            if m >= ITEMS - NARROW_TAIL:
-                return (m, 1)
-            return (m - G + 1, G) if m % G == G - 1 else None
+        def mix_first(b):
+            if b is not None:
+                mix_sub(b, 0, 2)
+                mix_sub(b, 2, 2)
 
-        ctx.enter_context(tc.manual_schedule(engines={mybir.EngineType.SP}))
-        load_w(0, R_GATE, (0,))
+        def mix_rest(b):
+            if b is not None:
+                mix_mul(b, 0, 2)
+                mix_mul(b, 2, 2)
+                mix_add(b, 0, 2)
+                mix_add(b, 2, 2)
+
+        def zc_block(b, prev, prep):
+            cb, nb = b
+            for ct in range(TILES):
+                z_product(cb, nb, ct)
+            mix_first(prev)
+            if prep is not None:
+                w_regroup(prep[0], prep[1])
+            for ct in range(TILES):
+                c_product(cb, nb, ct)
+            mix_rest(prev)
+            if prep is not None:
+                w_quantise(prep[0], prep[1])
+            turn_backs(cb, nb)
+
+        def r_phase(cb, prev, prep):
+            for nt in range(TILES):
+                r_product(cb, nt)
+            mix_first(prev)
+            if prep is not None:
+                w_regroup(prep[0], prep[1])
+            for nt in range(TILES, 2 * TILES):
+                r_product(cb, nt)
+            mix_rest(prev)
+            if prep is not None:
+                w_quantise(prep[0], prep[1])
+            for nb in range(2):
+                for ct in range(TILES):
+                    r_turn(cb, nb, ct)
+
+        pinned = {mybir.EngineType.SP}
+        for e in PIN:
+            pinned.add(e)
+        ctx.enter_context(tc.manual_schedule(engines=pinned))
         load_h(0)
-        load_w(0, R_GATE, (1,))
-        load_x(0)
-        load_x(1)
+        load_w(0, R_GATE, (0,))
         load_h(1)
-        load_w(0, Z_GATE)
-        load_x(2)
-        load_x(3)
-        load_w(0, C_GATE)
+        load_w(0, R_GATE, (1,))
         load_h(2)
-        load_x(4)
-        load_x(5)
         load_h(3)
-        load_x(6)
-        load_x(7)
+        load_x(0, R_GATE, 0)
+        load_x(0, R_GATE, 1)
+        load_w(0, Z_GATE)
+        load_w(0, C_GATE)
+        for nb in range(2):
+            load_x(0, Z_GATE, nb)
+            load_x(0, C_GATE, nb)
         load_w(1, R_GATE)
+        load_x(1, R_GATE, 0)
+        load_x(1, R_GATE, 1)
         load_w(1, Z_GATE)
         load_w(1, C_GATE)
-        for i in range(8, ITEMS):
-            load_x(i)
+        for nb in range(2):
+            load_x(1, Z_GATE, nb)
+            load_x(1, C_GATE, nb)
+
         h_transposes(0)
         w_regroup(0, R_GATE)
         h_quantise(0)
+        h_transposes(1)
         w_quantise(0, R_GATE)
-
-        def turn_run(tick):
-            if is_item(tick - C_TURN_LAG):
-                c_turn(tick - C_TURN_LAG)
-            if is_item(tick - Z_TURN_LAG):
-                z_turn(tick - Z_TURN_LAG)
-            if is_item(tick - R_TURN_LAG):
-                r_turn(tick - R_TURN_LAG)
-            if tick in H_PREP:
-                h_transposes(H_PREP[tick])
-
-        def mx_run(tick):
-            if is_item(tick):
-                r_product(tick)
-            if is_item(tick - C_MX_LAG):
-                c_product(tick - C_MX_LAG)
-            if is_item(tick - Z_MX_LAG):
-                z_product(tick - Z_MX_LAG)
-
-        for tick in range(ITEMS + MIX_LAG + 3):
-            if ALTERNATE and tick % 2 == 1:
-                mx_run(tick)
-                turn_run(tick)
-            else:
-                turn_run(tick)
-                mx_run(tick)
-            m = tick - MIX_LAG
-            if tick in W_PREP:
-                w_regroup(W_PREP[tick][0], W_PREP[tick][1])
-            if mix_work(m) is not None:
-                mix_sub(mix_work(m)[0], mix_work(m)[1])
-            if is_item(tick - C_MUL_LAG):
-                c_multiply(tick - C_MUL_LAG)
-            if mix_work(m - 1) is not None:
-                mix_mul(mix_work(m - 1)[0], mix_work(m - 1)[1])
-            if is_item(tick - R_ADD_LAG):
-                r_add(tick - R_ADD_LAG)
-            if mix_work(m - 2) is not None:
-                mix_add(mix_work(m - 2)[0], mix_work(m - 2)[1])
-            if tick in H_PREP:
-                h_quantise(H_PREP[tick])
-            if tick in W_PREP:
-                w_quantise(W_PREP[tick][0], W_PREP[tick][1])
+        h_quantise(1)
+        h_transposes(2)
+        h_transposes(3)
+        for nt in range(TILES):
+            r_product(0, nt)
+        h_quantise(2)
+        w_regroup(0, Z_GATE)
+        h_quantise(3)
+        w_quantise(0, Z_GATE)
+        for nt in range(TILES, 2 * TILES):
+            r_product(0, nt)
+        w_regroup(0, C_GATE)
+        for ct in range(TILES):
+            r_turn(0, 0, ct)
+        w_quantise(0, C_GATE)
+        for ct in range(TILES):
+            r_turn(0, 1, ct)
+        zc_block((0, 0), None, (1, R_GATE))
+        zc_block((0, 1), (0, 0), (1, Z_GATE))
+        r_phase(1, (0, 1), (1, C_GATE))
+        zc_block((1, 0), None, None)
+        zc_block((1, 1), (1, 0), None)
+        last = (1, 1)
+        for j0 in (0, 2):
+            mix_sub(last, j0, 1)
+            mix_sub(last, j0 + 1, 1)
+            mix_mul(last, j0, 1)
+            mix_mul(last, j0 + 1, 1)
+            mix_add(last, j0, 1)
+            mix_add(last, j0 + 1, 1)

@@ -29,7 +29,7 @@ ON_SCALAR = (
     (0, Z_GATE, 1), (0, C_GATE, 1), (1, R_GATE, 1), (1, Z_GATE, 1), (1, C_GATE, 1),
 )
 IDS_TOGETHER = False
-PIN = ()
+PIN = (mybir.EngineType.PE, mybir.EngineType.DVE, mybir.EngineType.Activation)
 
 
 def tile_gatedgraphconvolution_pb_kernel(
@@ -42,8 +42,9 @@ def tile_gatedgraphconvolution_pb_kernel(
     with ExitStack() as ctx:
         const = ctx.enter_context(tc.tile_pool(name="const", bufs=1))
         keep = ctx.enter_context(tc.tile_pool(name="keep", bufs=1))
+        w_q_pool = ctx.enter_context(tc.tile_pool(name="w_q", bufs=4))
         w_raw_pool = ctx.enter_context(tc.tile_pool(name="w_raw", bufs=6))
-        grouped_pool = ctx.enter_context(tc.tile_pool(name="grouped", bufs=3))
+        grouped_pool = ctx.enter_context(tc.tile_pool(name="grouped", bufs=4))
         h_grouped_pool = ctx.enter_context(tc.tile_pool(name="h_grouped", bufs=4))
         x_pool = ctx.enter_context(tc.tile_pool(name="x", bufs=8))
         ar_pool = ctx.enter_context(tc.tile_pool(name="ar", bufs=8))
@@ -52,7 +53,7 @@ def tile_gatedgraphconvolution_pb_kernel(
         zb_pool = ctx.enter_context(tc.tile_pool(name="zb", bufs=6))
         cand_pool = ctx.enter_context(tc.tile_pool(name="cand", bufs=4))
         z_pool = ctx.enter_context(tc.tile_pool(name="z", bufs=4))
-        mix_pool = ctx.enter_context(tc.tile_pool(name="mix", bufs=3))
+        mix_pool = ctx.enter_context(tc.tile_pool(name="mix", bufs=4))
         psum = ctx.enter_context(tc.psum_pool(name="psum", bufs=8))
 
         def bank(shape, dtype=F32):
@@ -81,12 +82,8 @@ def tile_gatedgraphconvolution_pb_kernel(
         h_sb = keep.tile([P, NODES // P, C], BF16, name="h_sb")
         h_codes = keep.tile([P, PASSES, NODES], U32, name="h_codes", align_bytes=64)
         h_scales = keep.tile([P, PASSES, NODES], U8, name="h_scales", align_bytes=64)
-        w_chunks = 2 * 3 * PASSES
-        w_codes = keep.tile([P, w_chunks, HALF], U32, name="w_codes", align_bytes=64)
-        w_scales = keep.tile([P, w_chunks, HALF], U8, name="w_scales", align_bytes=64)
-
-        def w_chunk(cb, gate, s):
-            return (cb * 3 + gate) * PASSES + s
+        w_codes = {}
+        w_scales = {}
 
         w_raw = {}
         x_tiles = {}
@@ -132,11 +129,12 @@ def tile_gatedgraphconvolution_pb_kernel(
                 grouped_w[(cb, gate, s)] = g_t
 
         def w_quantise(cb, gate):
+            w_codes[(cb, gate)] = w_q_pool.tile([P, PASSES, HALF], U32, name="w_codes", tag="w_codes", align_bytes=64)
+            w_scales[(cb, gate)] = w_q_pool.tile([P, PASSES, HALF], U8, name="w_scales", tag="w_scales", align_bytes=64)
             for s in range(PASSES):
-                chunk = w_chunk(cb, gate, s)
                 nc.vector.quantize_mx(
-                    out=w_codes[:, chunk, :].bitcast(FP8X4),
-                    scales=w_scales[:, chunk, :],
+                    out=w_codes[(cb, gate)][:, s, :].bitcast(FP8X4),
+                    scales=w_scales[(cb, gate)][:, s, :],
                     in_=grouped_w[(cb, gate, s)][:],
                 )
 
@@ -171,13 +169,12 @@ def tile_gatedgraphconvolution_pb_kernel(
         def mx_nodes_out(bk, cb, gate, nt):
             nodes = slice(nt * P, (nt + 1) * P)
             for s in range(PASSES):
-                chunk = w_chunk(cb, gate, s)
                 nc.tensor.matmul_mx(
                     out=bk[:],
                     lhsT=h_codes[:, s, nodes].bitcast(FP8X4),
                     lhsT_scale=h_scales[:, s, nodes],
-                    rhs=w_codes[:, chunk, :].bitcast(FP8X4),
-                    rhs_scale=w_scales[:, chunk, :],
+                    rhs=w_codes[(cb, gate)][:, s, :].bitcast(FP8X4),
+                    rhs_scale=w_scales[(cb, gate)][:, s, :],
                     start=(s == 0),
                     stop=(s == PASSES - 1),
                 )
@@ -186,11 +183,10 @@ def tile_gatedgraphconvolution_pb_kernel(
             nodes = slice(nb * HALF, (nb + 1) * HALF)
             cols = slice(ct * P, (ct + 1) * P)
             for s in range(PASSES):
-                chunk = w_chunk(cb, gate, s)
                 nc.tensor.matmul_mx(
                     out=bk[:],
-                    lhsT=w_codes[:, chunk, cols].bitcast(FP8X4),
-                    lhsT_scale=w_scales[:, chunk, cols],
+                    lhsT=w_codes[(cb, gate)][:, s, cols].bitcast(FP8X4),
+                    lhsT_scale=w_scales[(cb, gate)][:, s, cols],
                     rhs=h_codes[:, s, nodes].bitcast(FP8X4),
                     rhs_scale=h_scales[:, s, nodes],
                     start=(s == 0),
@@ -304,7 +300,7 @@ def tile_gatedgraphconvolution_pb_kernel(
                 mixes[w][:, k : k + count, :],
                 h_sb[:, nt : nt + count, cols],
                 cand[w][:, k : k + count, :],
-                z_tiles[w][:, k : k + count, :],
+                z_tiles[w][:, k : k + count, :] if w in z_tiles else None,
                 out_rows[nt * P : (nt + count) * P, cols].rearrange("(t p) c -> p t c", p=P),
             )
 
@@ -335,60 +331,80 @@ def tile_gatedgraphconvolution_pb_kernel(
                 mix_add(b, 0, 2)
                 mix_add(b, 2, 2)
 
-        def zc_block(b, prev, prep):
+        def last_turn_backs(cb, nb):
+            b = (cb, nb)
+            cbk = [back_open(cb, C_GATE, nb, j) for j in range(TILES)]
+            for j in range(TILES):
+                back_turn(cbk[j], mt, cb, nb, j)
+                finish(cbk[j], cand, cand_pool, "cand", ACT.Tanh, cb, nb, j)
+            zbk = [back_open(cb, Z_GATE, nb, j) for j in range(TILES)]
+            for j in range(TILES):
+                mix_sub(b, j, 1)
+            for j in range(TILES):
+                back_turn(zbk[j], zb, cb, nb, j)
+                finish(zbk[j], z_tiles, z_pool, "z", ACT.Sigmoid, cb, nb, j)
+            for j0 in (0, 2):
+                mix_mul(b, j0, 1)
+                mix_mul(b, j0 + 1, 1)
+                mix_add(b, j0, 1)
+                mix_add(b, j0 + 1, 1)
+
+        def period(b, prev, nxt, prep, is_last=False):
             cb, nb = b
             for ct in range(TILES):
                 z_product(cb, nb, ct)
-            mix_first(prev)
-            if prep is not None:
-                w_regroup(prep[0], prep[1])
+            if prev is not None:
+                mix_sub(prev, 0, 2)
+                mix_sub(prev, 2, 2)
+                mix_mul(prev, 0, 2)
+                mix_mul(prev, 2, 2)
             for ct in range(TILES):
                 c_product(cb, nb, ct)
-            mix_rest(prev)
-            if prep is not None:
-                w_quantise(prep[0], prep[1])
-            turn_backs(cb, nb)
-
-        def r_phase(cb, prev, prep):
-            for nt in range(TILES):
-                r_product(cb, nt)
-            mix_first(prev)
-            if prep is not None:
-                w_regroup(prep[0], prep[1])
-            for nt in range(TILES, 2 * TILES):
-                r_product(cb, nt)
-            mix_rest(prev)
-            if prep is not None:
-                w_quantise(prep[0], prep[1])
-            for nb in range(2):
+            for g in prep:
+                w_regroup(g[0], g[1])
+            if nxt is not None:
+                for j in range(TILES):
+                    r_product(nxt[0], nxt[1] * TILES + j)
+            if prev is not None:
+                mix_add(prev, 0, 2)
+                mix_add(prev, 2, 2)
+            for g in prep:
+                w_quantise(g[0], g[1])
+            if is_last:
+                last_turn_backs(cb, nb)
+            else:
+                turn_backs(cb, nb)
+            if nxt is not None:
                 for ct in range(TILES):
-                    r_turn(cb, nb, ct)
+                    r_turn(nxt[0], nxt[1], ct)
 
         pinned = {mybir.EngineType.SP}
         for e in PIN:
             pinned.add(e)
         ctx.enter_context(tc.manual_schedule(engines=pinned))
-        load_h(0)
         load_w(0, R_GATE, (0,))
-        load_h(1)
+        load_h(0)
         load_w(0, R_GATE, (1,))
-        load_h(2)
-        load_h(3)
+        load_h(1)
         load_x(0, R_GATE, 0)
-        load_x(0, R_GATE, 1)
         load_w(0, Z_GATE)
         load_w(0, C_GATE)
-        for nb in range(2):
-            load_x(0, Z_GATE, nb)
-            load_x(0, C_GATE, nb)
+        load_h(2)
+        load_h(3)
+        load_x(0, Z_GATE, 0)
+        load_x(0, C_GATE, 0)
+        load_x(0, R_GATE, 1)
         load_w(1, R_GATE)
+        load_x(0, Z_GATE, 1)
+        load_x(0, C_GATE, 1)
         load_x(1, R_GATE, 0)
-        load_x(1, R_GATE, 1)
         load_w(1, Z_GATE)
         load_w(1, C_GATE)
-        for nb in range(2):
-            load_x(1, Z_GATE, nb)
-            load_x(1, C_GATE, nb)
+        load_x(1, Z_GATE, 0)
+        load_x(1, C_GATE, 0)
+        load_x(1, R_GATE, 1)
+        load_x(1, Z_GATE, 1)
+        load_x(1, C_GATE, 1)
 
         h_transposes(0)
         w_regroup(0, R_GATE)
@@ -396,32 +412,19 @@ def tile_gatedgraphconvolution_pb_kernel(
         h_transposes(1)
         w_quantise(0, R_GATE)
         h_quantise(1)
-        h_transposes(2)
-        h_transposes(3)
         for nt in range(TILES):
             r_product(0, nt)
-        h_quantise(2)
         w_regroup(0, Z_GATE)
-        h_quantise(3)
-        w_quantise(0, Z_GATE)
-        for nt in range(TILES, 2 * TILES):
-            r_product(0, nt)
-        w_regroup(0, C_GATE)
         for ct in range(TILES):
             r_turn(0, 0, ct)
+        w_quantise(0, Z_GATE)
+        h_transposes(2)
+        w_regroup(0, C_GATE)
+        h_transposes(3)
+        h_quantise(2)
         w_quantise(0, C_GATE)
-        for ct in range(TILES):
-            r_turn(0, 1, ct)
-        zc_block((0, 0), None, (1, R_GATE))
-        zc_block((0, 1), (0, 0), (1, Z_GATE))
-        r_phase(1, (0, 1), (1, C_GATE))
-        zc_block((1, 0), None, None)
-        zc_block((1, 1), (1, 0), None)
-        last = (1, 1)
-        for j0 in (0, 2):
-            mix_sub(last, j0, 1)
-            mix_sub(last, j0 + 1, 1)
-            mix_mul(last, j0, 1)
-            mix_mul(last, j0 + 1, 1)
-            mix_add(last, j0, 1)
-            mix_add(last, j0 + 1, 1)
+        h_quantise(3)
+        period((0, 0), None, (0, 1), ((1, R_GATE),))
+        period((0, 1), (0, 0), (1, 0), ((1, Z_GATE), (1, C_GATE)))
+        period((1, 0), (0, 1), (1, 1), ())
+        period((1, 1), (1, 0), None, (), True)

@@ -29,7 +29,8 @@ ON_SCALAR = (
     (0, Z_GATE, 1), (0, C_GATE, 1), (1, R_GATE, 1), (1, Z_GATE, 1), (1, C_GATE, 1),
 )
 IDS_TOGETHER = False
-PIN = (mybir.EngineType.PE, mybir.EngineType.DVE, mybir.EngineType.Activation)
+G_ITEMS = 2
+PIN = (mybir.EngineType.PE, mybir.EngineType.DVE, mybir.EngineType.Activation, mybir.EngineType.Pool)
 
 
 def tile_gatedgraphconvolution_pb_kernel(
@@ -319,6 +320,11 @@ def tile_gatedgraphconvolution_pb_kernel(
             nc.vector.tensor_add(out=m_ap, in0=m_ap, in1=c_ap)
             nc.sync.dma_start(out=o_ap, in_=m_ap)
 
+        def mix_add_pool(b, j, count):
+            m_ap, h_ap, c_ap, z_ap, o_ap = span(b, j, count)
+            nc.gpsimd.tensor_tensor(out=m_ap, in0=m_ap, in1=c_ap, op=ALU.add)
+            nc.sync.dma_start(out=o_ap, in_=m_ap)
+
         def mix_first(b):
             if b is not None:
                 mix_sub(b, 0, 2)
@@ -358,16 +364,19 @@ def tile_gatedgraphconvolution_pb_kernel(
                 mix_sub(prev, 2, 2)
                 mix_mul(prev, 0, 2)
                 mix_mul(prev, 2, 2)
+                for j in range(0, TILES, G_ITEMS):
+                    mix_add_pool(prev, j, G_ITEMS)
             for ct in range(TILES):
                 c_product(cb, nb, ct)
-            for g in prep:
-                w_regroup(g[0], g[1])
+            if prev is None:
+                for g in prep:
+                    w_regroup(g[0], g[1])
             if nxt is not None:
                 for j in range(TILES):
                     r_product(nxt[0], nxt[1] * TILES + j)
             if prev is not None:
-                mix_add(prev, 0, 2)
-                mix_add(prev, 2, 2)
+                for g in prep:
+                    w_regroup(g[0], g[1])
             for g in prep:
                 w_quantise(g[0], g[1])
             if is_last:

@@ -29,7 +29,6 @@ ON_SCALAR = (
     (0, Z_GATE, 1), (0, C_GATE, 1), (1, R_GATE, 1), (1, Z_GATE, 1), (1, C_GATE, 1),
 )
 IDS_TOGETHER = False
-G_ITEMS = 2
 PIN = (mybir.EngineType.PE, mybir.EngineType.DVE, mybir.EngineType.Activation, mybir.EngineType.Pool)
 
 
@@ -364,10 +363,13 @@ def tile_gatedgraphconvolution_pb_kernel(
                 mix_sub(prev, 2, 2)
                 mix_mul(prev, 0, 2)
                 mix_mul(prev, 2, 2)
-                for j in range(0, TILES, G_ITEMS):
-                    mix_add_pool(prev, j, G_ITEMS)
+                mix_add_pool(prev, 0, 2)
+                if not is_last:
+                    mix_add_pool(prev, 2, 2)
             for ct in range(TILES):
                 c_product(cb, nb, ct)
+            if is_last:
+                mix_add(prev, 2, 2)
             if prev is None:
                 for g in prep:
                     w_regroup(g[0], g[1])

@@ -25,9 +25,9 @@ Z_GATE, R_GATE, C_GATE = 0, 1, 2
 FLOPS = 2 * NODES * C * 3 * C
 
 S_PIECES = 4
-ON_SCALAR = (
-    (0, Z_GATE, 1), (0, C_GATE, 1), (1, R_GATE, 1), (1, Z_GATE, 1), (1, C_GATE, 1),
-)
+ON_SCALAR = ((0, Z_GATE, 1), (0, C_GATE, 1), (1, Z_GATE, 1), (1, C_GATE, 1))
+ON_GPSIMD = ((1, R_GATE, 1),)
+G_PIECES = 4
 IDS_TOGETHER = False
 PIN = (mybir.EngineType.PE, mybir.EngineType.DVE, mybir.EngineType.Activation, mybir.EngineType.Pool)
 
@@ -124,6 +124,14 @@ def tile_gatedgraphconvolution_pb_kernel(
                     for piece in range(S_PIECES):
                         part = slice(piece * step, (piece + 1) * step)
                         nc.scalar.copy(out=dst[:, part, :, :], in_=src[:, part, :, :])
+                elif (cb, gate, s) in ON_GPSIMD:
+                    step = HALF // 4 // G_PIECES
+                    for piece in range(G_PIECES):
+                        part = slice(piece * step, (piece + 1) * step)
+                        nc.gpsimd.tensor_scalar(
+                            out=dst[:, part, :, :], in0=src[:, part, :, :],
+                            scalar1=1.0, scalar2=0.0, op0=ALU.mult, op1=ALU.add,
+                        )
                 else:
                     nc.vector.tensor_copy(out=dst, in_=src)
                 grouped_w[(cb, gate, s)] = g_t

@@ -25,7 +25,7 @@ Z_GATE, R_GATE, C_GATE = 0, 1, 2
 FLOPS = 2 * NODES * C * 3 * C
 
 S_PIECES = 4
-ON_SCALAR = ((0, Z_GATE, 1), (0, C_GATE, 1), (1, Z_GATE, 1), (1, C_GATE, 1))
+ON_SCALAR = ((0, Z_GATE, 1), (1, Z_GATE, 1), (1, C_GATE, 1))
 ON_GPSIMD = ((1, R_GATE, 1),)
 G_PIECES = 4
 IDS_TOGETHER = False

@@ -29,7 +29,7 @@ ON_SCALAR = ((0, Z_GATE, 1), (1, Z_GATE, 1), (1, C_GATE, 1))
 ON_GPSIMD = ((1, R_GATE, 1),)
 G_PIECES = 4
 IDS_TOGETHER = False
-PIN = (mybir.EngineType.PE, mybir.EngineType.DVE, mybir.EngineType.Activation, mybir.EngineType.Pool)
+PIN = (mybir.EngineType.DVE, mybir.EngineType.Activation, mybir.EngineType.Pool)
 
 
 def tile_gatedgraphconvolution_pb_kernel(

from contextlib import ExitStack

import concourse.mybir as mybir
from concourse.masks import make_identity

F32 = mybir.dt.float32
BF16 = mybir.dt.bfloat16
U32 = mybir.dt.uint32
U8 = mybir.dt.uint8
FP8X4 = mybir.dt.float8_e4m3fn_x4
ACT = mybir.ActivationFunctionType
ALU = mybir.AluOpType

P = 128
PACK = 4
K_PASS = P * PACK
NODES = 1024
C = 1024
PASSES = C // K_PASS
HALF = 512
TILES = HALF // P

Z_GATE, R_GATE, C_GATE = 0, 1, 2

FLOPS = 2 * NODES * C * 3 * C

S_PIECES = 4
ON_SCALAR = ((0, Z_GATE, 1), (1, Z_GATE, 1), (1, C_GATE, 1))
ON_GPSIMD = ((1, R_GATE, 1),)
G_PIECES = 4
IDS_TOGETHER = False
PIN = (mybir.EngineType.DVE, mybir.EngineType.Activation, mybir.EngineType.Pool)


def tile_gatedgraphconvolution_pb_kernel(
    tc, x_proj, annotations, recurrent_kernel, bias_h, out
):
    nc = tc.nc
    h_rows = annotations.flatten_outer_dims()
    out_rows = out.flatten_outer_dims()

    with ExitStack() as ctx:
        const = ctx.enter_context(tc.tile_pool(name="const", bufs=1))
        keep = ctx.enter_context(tc.tile_pool(name="keep", bufs=1))
        w_q_pool = ctx.enter_context(tc.tile_pool(name="w_q", bufs=4))
        w_raw_pool = ctx.enter_context(tc.tile_pool(name="w_raw", bufs=6))
        grouped_pool = ctx.enter_context(tc.tile_pool(name="grouped", bufs=4))
        h_grouped_pool = ctx.enter_context(tc.tile_pool(name="h_grouped", bufs=4))
        x_pool = ctx.enter_context(tc.tile_pool(name="x", bufs=8))
        ar_pool = ctx.enter_context(tc.tile_pool(name="ar", bufs=8))
        rt_pool = ctx.enter_context(tc.tile_pool(name="rt", bufs=8))
        mt_pool = ctx.enter_context(tc.tile_pool(name="mt", bufs=6))
        zb_pool = ctx.enter_context(tc.tile_pool(name="zb", bufs=6))
        cand_pool = ctx.enter_context(tc.tile_pool(name="cand", bufs=4))
        z_pool = ctx.enter_context(tc.tile_pool(name="z", bufs=4))
        mix_pool = ctx.enter_context(tc.tile_pool(name="mix", bufs=4))
        psum = ctx.enter_context(tc.psum_pool(name="psum", bufs=8))

        def bank(shape, dtype=F32):
            return psum.tile(shape, dtype, name="bank", tag="bank")

        ident_f32 = const.tile([P, P], F32, name="ident_f32")
        make_identity(nc, ident_f32[:])
        ident_bf16 = const.tile([P, P], BF16, name="ident_bf16")
        make_identity(nc, ident_bf16[:])

        warm = const.tile([P, 1], F32, name="warm")
        nc.vector.memset(warm[:], 0.0)
        nc.scalar.activation(out=warm[:], in_=warm[:], func=ACT.Sigmoid)

        bias_tiles = 3 * C // P
        bias_rows = const.tile([P, P], BF16, name="bias_rows")
        nc.vector.memset(bias_rows[:], 0.0)
        nc.sync.dma_start(
            out=bias_rows[0:bias_tiles, :], in_=bias_h.rearrange("(j p) -> j p", p=P)
        )
        bias_turned = bank([P, P], BF16)
        nc.tensor.transpose(out=bias_turned[:], in_=bias_rows[:], identity=ident_bf16[:])
        bias_col = const.tile([P, bias_tiles], F32, name="bias_col")
        nc.vector.tensor_copy(out=bias_col[:], in_=bias_turned[:, 0:bias_tiles])

        h_sb = keep.tile([P, NODES // P, C], BF16, name="h_sb")
        h_codes = keep.tile([P, PASSES, NODES], U32, name="h_codes", align_bytes=64)
        h_scales = keep.tile([P, PASSES, NODES], U8, name="h_scales", align_bytes=64)
        w_codes = {}
        w_scales = {}

        w_raw = {}
        x_tiles = {}
        grouped_w = {}
        grouped_h = {}

        def load_w(cb, gate, passes=(0, 1)):
            col0 = gate * C + cb * HALF
            for s in passes:
                raw = w_raw_pool.tile([P, PACK, HALF], BF16, name="w_raw", tag="w_raw")
                rows = recurrent_kernel[s * K_PASS : (s + 1) * K_PASS, col0 : col0 + HALF]
                nc.sync.dma_start(out=raw[:], in_=rows.rearrange("(p t) c -> p t c", t=PACK))
                w_raw[(cb, gate, s)] = raw

        def load_h(hg):
            nt0 = 2 * hg
            rows = h_rows[nt0 * P : (nt0 + 2) * P, :]
            nc.sync.dma_start(
                out=h_sb[:, nt0 : nt0 + 2, :], in_=rows.rearrange("(t p) c -> p t c", p=P)
            )

        def load_x(cb, gate, nb):
            x_t = x_pool.tile([P, TILES, HALF], BF16, name="x_t", tag="x_t")
            col0 = gate * C + cb * HALF
            rows = x_proj[nb * HALF : (nb + 1) * HALF, col0 : col0 + HALF]
            nc.sync.dma_start(out=x_t[:], in_=rows.rearrange("(j p) c -> p j c", p=P))
            x_tiles[(cb, gate, nb)] = x_t

        def w_regroup(cb, gate):
            for s in range(PASSES):
                g_t = grouped_pool.tile(
                    [P, HALF * PACK], BF16, name="grouped", tag="grouped", align_bytes=64
                )
                dst = g_t[:].rearrange("p (c i t) -> p c t i", i=4, t=PACK)
                src = w_raw[(cb, gate, s)][:].rearrange("p t (c i) -> p c t i", i=4)
                if (cb, gate, s) in ON_SCALAR:
                    step = HALF // 4 // S_PIECES
                    for piece in range(S_PIECES):
                        part = slice(piece * step, (piece + 1) * step)
                        nc.scalar.copy(out=dst[:, part, :, :], in_=src[:, part, :, :])
                elif (cb, gate, s) in ON_GPSIMD:
                    step = HALF // 4 // G_PIECES
                    for piece in range(G_PIECES):
                        part = slice(piece * step, (piece + 1) * step)
                        nc.gpsimd.tensor_scalar(
                            out=dst[:, part, :, :], in0=src[:, part, :, :],
                            scalar1=1.0, scalar2=0.0, op0=ALU.mult, op1=ALU.add,
                        )
                else:
                    nc.vector.tensor_copy(out=dst, in_=src)
                grouped_w[(cb, gate, s)] = g_t

        def w_quantise(cb, gate):
            w_codes[(cb, gate)] = w_q_pool.tile([P, PASSES, HALF], U32, name="w_codes", tag="w_codes", align_bytes=64)
            w_scales[(cb, gate)] = w_q_pool.tile([P, PASSES, HALF], U8, name="w_scales", tag="w_scales", align_bytes=64)
            for s in range(PASSES):
                nc.vector.quantize_mx(
                    out=w_codes[(cb, gate)][:, s, :].bitcast(FP8X4),
                    scales=w_scales[(cb, gate)][:, s, :],
                    in_=grouped_w[(cb, gate, s)][:],
                )

        def h_transposes(hg):
            for s in range(PASSES):
                grouped_h[(hg, s)] = h_grouped_pool.tile(
                    [P, 2 * P * PACK], BF16, name="h_grouped", tag="h_grouped", align_bytes=64
                )
                g_words = grouped_h[(hg, s)][:].bitcast(F32).rearrange("p (n u) -> p n u", u=2)
                h_turned = bank([P, 2, 2 * P])
                for j in range(2):
                    words = h_sb[:, 2 * hg + j, :].bitcast(F32).rearrange(
                        "p (s w u) -> p s u w", s=PASSES, u=2
                    )
                    for u in range(2):
                        nc.tensor.transpose(
                            out=h_turned[:, u, j * P : (j + 1) * P],
                            in_=words[:, s, u, :],
                            identity=ident_f32[:],
                        )
                nc.scalar.copy(out=g_words, in_=h_turned[:].rearrange("p u n -> p n u"))

        def h_quantise(hg):
            nodes = slice(hg * 2 * P, (hg + 1) * 2 * P)
            for s in range(PASSES):
                nc.vector.quantize_mx(
                    out=h_codes[:, s, nodes].bitcast(FP8X4),
                    scales=h_scales[:, s, nodes],
                    in_=grouped_h[(hg, s)][:],
                )

        def mx_nodes_out(bk, cb, gate, nt):
            nodes = slice(nt * P, (nt + 1) * P)
            for s in range(PASSES):
                nc.tensor.matmul_mx(
                    out=bk[:],
                    lhsT=h_codes[:, s, nodes].bitcast(FP8X4),
                    lhsT_scale=h_scales[:, s, nodes],
                    rhs=w_codes[(cb, gate)][:, s, :].bitcast(FP8X4),
                    rhs_scale=w_scales[(cb, gate)][:, s, :],
                    start=(s == 0),
                    stop=(s == PASSES - 1),
                )

        def mx_cols_out(bk, cb, gate, ct, nb):
            nodes = slice(nb * HALF, (nb + 1) * HALF)
            cols = slice(ct * P, (ct + 1) * P)
            for s in range(PASSES):
                nc.tensor.matmul_mx(
                    out=bk[:],
                    lhsT=w_codes[(cb, gate)][:, s, cols].bitcast(FP8X4),
                    lhsT_scale=w_scales[(cb, gate)][:, s, cols],
                    rhs=h_codes[:, s, nodes].bitcast(FP8X4),
                    rhs_scale=h_scales[:, s, nodes],
                    start=(s == 0),
                    stop=(s == PASSES - 1),
                )

        def bias_of(gate, cb, ct):
            j = gate * (C // P) + cb * TILES + ct
            return bias_col[:, j : j + 1]

        ar = {}
        rt = {}
        mt = {}
        zb = {}
        cand = {}
        z_tiles = {}
        mixes = {}

        def r_product(cb, nt):
            nb, j = divmod(nt, TILES)
            bk = bank([P, HALF])
            mx_nodes_out(bk, cb, R_GATE, nt)
            ar[(cb, nt)] = ar_pool.tile([P, HALF], F32, name="ar", tag="ar")
            nc.vector.tensor_add(out=ar[(cb, nt)][:], in0=bk[:], in1=x_tiles[(cb, R_GATE, nb)][:, j, :])

        def r_turn(cb, nb, ct):
            bk = bank([P, HALF])
            for j in range(TILES):
                nc.tensor.matmul(
                    out=bk[:, j * P : (j + 1) * P],
                    lhsT=ar[(cb, nb * TILES + j)][:, ct * P : (ct + 1) * P],
                    rhs=ident_f32[:],
                    is_transpose=True,
                    start=True,
                    stop=True,
                )
            rt[(cb, nb, ct)] = rt_pool.tile([P, HALF], F32, name="rt", tag="rt")
            nc.scalar.activation(
                out=rt[(cb, nb, ct)][:], in_=bk[:], func=ACT.Sigmoid,
                bias=bias_of(R_GATE, cb, ct), scale=1.0,
            )

        def z_product(cb, nb, ct):
            bk = bank([P, HALF])
            mx_cols_out(bk, cb, Z_GATE, ct, nb)
            zb[(cb, nb, ct)] = zb_pool.tile([P, HALF], F32, name="zb", tag="zb")
            nc.scalar.activation(
                out=zb[(cb, nb, ct)][:], in_=bk[:], func=ACT.Identity,
                bias=bias_of(Z_GATE, cb, ct), scale=1.0,
            )

        def c_product(cb, nb, ct):
            bk = bank([P, HALF])
            mx_cols_out(bk, cb, C_GATE, ct, nb)
            mt[(cb, nb, ct)] = mt_pool.tile([P, HALF], F32, name="mt", tag="mt")
            nc.vector.scalar_tensor_tensor(
                out=mt[(cb, nb, ct)][:],
                in0=bk[:],
                scalar=bias_of(C_GATE, cb, ct),
                in1=rt[(cb, nb, ct)][:],
                op0=ALU.add,
                op1=ALU.mult,
            )

        def back_open(cb, gate, nb, j):
            bk = bank([P, HALF])
            nc.tensor.matmul(
                out=bk[:], lhsT=ident_bf16[:], rhs=x_tiles[(cb, gate, nb)][:, j, :],
                start=True, stop=False,
            )
            return bk

        def back_turn(bk, tiles, cb, nb, j):
            for ct in range(TILES):
                nc.tensor.matmul(
                    out=bk[:, ct * P : (ct + 1) * P],
                    lhsT=tiles[(cb, nb, ct)][:, j * P : (j + 1) * P],
                    rhs=ident_f32[:],
                    is_transpose=True,
                    start=False,
                    stop=ct == TILES - 1,
                )

        def finish(bk, store, pool, name, func, cb, nb, j):
            if j % 2 == 0:
                store[(cb, nb, j // 2)] = pool.tile([P, 2, HALF], F32, name=name, tag=name)
            nc.scalar.activation(out=store[(cb, nb, j // 2)][:, j % 2, :], in_=bk[:], func=func)

        def turn_backs(cb, nb):
            if IDS_TOGETHER:
                zbk = [back_open(cb, Z_GATE, nb, j) for j in range(TILES)]
                cbk = [back_open(cb, C_GATE, nb, j) for j in range(TILES)]
            else:
                zbk = [back_open(cb, Z_GATE, nb, j) for j in range(TILES)]
            for j in range(TILES):
                back_turn(zbk[j], zb, cb, nb, j)
                finish(zbk[j], z_tiles, z_pool, "z", ACT.Sigmoid, cb, nb, j)
            if not IDS_TOGETHER:
                cbk = [back_open(cb, C_GATE, nb, j) for j in range(TILES)]
            for j in range(TILES):
                back_turn(cbk[j], mt, cb, nb, j)
                finish(cbk[j], cand, cand_pool, "cand", ACT.Tanh, cb, nb, j)

        def span(b, j, count):
            cb, nb = b
            w = (cb, nb, j // 2)
            nt = nb * TILES + j
            cols = slice(cb * HALF, (cb + 1) * HALF)
            k = j % 2
            return (
                mixes[w][:, k : k + count, :],
                h_sb[:, nt : nt + count, cols],
                cand[w][:, k : k + count, :],
                z_tiles[w][:, k : k + count, :] if w in z_tiles else None,
                out_rows[nt * P : (nt + count) * P, cols].rearrange("(t p) c -> p t c", p=P),
            )

        def mix_sub(b, j, count):
            if j % 2 == 0:
                mixes[(b[0], b[1], j // 2)] = mix_pool.tile([P, 2, HALF], F32, name="mix", tag="mix")
            m_ap, h_ap, c_ap, z_ap, o_ap = span(b, j, count)
            nc.vector.tensor_sub(out=m_ap, in0=h_ap, in1=c_ap)

        def mix_mul(b, j, count):
            m_ap, h_ap, c_ap, z_ap, o_ap = span(b, j, count)
            nc.vector.tensor_mul(out=m_ap, in0=m_ap, in1=z_ap)

        def mix_add(b, j, count):
            m_ap, h_ap, c_ap, z_ap, o_ap = span(b, j, count)
            nc.vector.tensor_add(out=m_ap, in0=m_ap, in1=c_ap)
            nc.sync.dma_start(out=o_ap, in_=m_ap)

        def mix_add_pool(b, j, count):
            m_ap, h_ap, c_ap, z_ap, o_ap = span(b, j, count)
            nc.gpsimd.tensor_tensor(out=m_ap, in0=m_ap, in1=c_ap, op=ALU.add)
            nc.sync.dma_start(out=o_ap, in_=m_ap)

        def mix_first(b):
            if b is not None:
                mix_sub(b, 0, 2)
                mix_sub(b, 2, 2)

        def mix_rest(b):
            if b is not None:
                mix_mul(b, 0, 2)
                mix_mul(b, 2, 2)
                mix_add(b, 0, 2)
                mix_add(b, 2, 2)

        def last_turn_backs(cb, nb):
            b = (cb, nb)
            cbk = [back_open(cb, C_GATE, nb, j) for j in range(TILES)]
            for j in range(TILES):
                back_turn(cbk[j], mt, cb, nb, j)
                finish(cbk[j], cand, cand_pool, "cand", ACT.Tanh, cb, nb, j)
            zbk = [back_open(cb, Z_GATE, nb, j) for j in range(TILES)]
            for j in range(TILES):
                mix_sub(b, j, 1)
            for j in range(TILES):
                back_turn(zbk[j], zb, cb, nb, j)
                finish(zbk[j], z_tiles, z_pool, "z", ACT.Sigmoid, cb, nb, j)
            for j0 in (0, 2):
                mix_mul(b, j0, 1)
                mix_mul(b, j0 + 1, 1)
                mix_add(b, j0, 1)
                mix_add(b, j0 + 1, 1)

        def period(b, prev, nxt, prep, is_last=False):
            cb, nb = b
            for ct in range(TILES):
                z_product(cb, nb, ct)
            if prev is not None:
                mix_sub(prev, 0, 2)
                mix_sub(prev, 2, 2)
                mix_mul(prev, 0, 2)
                mix_mul(prev, 2, 2)
                mix_add_pool(prev, 0, 2)
                if not is_last:
                    mix_add_pool(prev, 2, 2)
            for ct in range(TILES):
                c_product(cb, nb, ct)
            if is_last:
                mix_add(prev, 2, 2)
            if prev is None:
                for g in prep:
                    w_regroup(g[0], g[1])
            if nxt is not None:
                for j in range(TILES):
                    r_product(nxt[0], nxt[1] * TILES + j)
            if prev is not None:
                for g in prep:
                    w_regroup(g[0], g[1])
            for g in prep:
                w_quantise(g[0], g[1])
            if is_last:
                last_turn_backs(cb, nb)
            else:
                turn_backs(cb, nb)
            if nxt is not None:
                for ct in range(TILES):
                    r_turn(nxt[0], nxt[1], ct)

        pinned = {mybir.EngineType.SP}
        for e in PIN:
            pinned.add(e)
        ctx.enter_context(tc.manual_schedule(engines=pinned))
        load_w(0, R_GATE, (0,))
        load_h(0)
        load_w(0, R_GATE, (1,))
        load_h(1)
        load_x(0, R_GATE, 0)
        load_w(0, Z_GATE)
        load_w(0, C_GATE)
        load_h(2)
        load_h(3)
        load_x(0, Z_GATE, 0)
        load_x(0, C_GATE, 0)
        load_x(0, R_GATE, 1)
        load_w(1, R_GATE)
        load_x(0, Z_GATE, 1)
        load_x(0, C_GATE, 1)
        load_x(1, R_GATE, 0)
        load_w(1, Z_GATE)
        load_w(1, C_GATE)
        load_x(1, Z_GATE, 0)
        load_x(1, C_GATE, 0)
        load_x(1, R_GATE, 1)
        load_x(1, Z_GATE, 1)
        load_x(1, C_GATE, 1)

        h_transposes(0)
        w_regroup(0, R_GATE)
        h_quantise(0)
        h_transposes(1)
        w_quantise(0, R_GATE)
        h_quantise(1)
        for nt in range(TILES):
            r_product(0, nt)
        w_regroup(0, Z_GATE)
        for ct in range(TILES):
            r_turn(0, 0, ct)
        w_quantise(0, Z_GATE)
        h_transposes(2)
        w_regroup(0, C_GATE)
        h_transposes(3)
        h_quantise(2)
        w_quantise(0, C_GATE)
        h_quantise(3)
        period((0, 0), None, (0, 1), ((1, R_GATE),))
        period((0, 1), (0, 0), (1, 0), ((1, Z_GATE), (1, C_GATE)))
        period((1, 0), (0, 1), (1, 1), ())
        period((1, 1), (1, 0), None, (), True)
